import numpy as np
import ml_dtypes


def mxq(x, axis, fmt="e4m3"):
    dtype, down = {"e4m3": (ml_dtypes.float8_e4m3fn, 7), "e5m2": (ml_dtypes.float8_e5m2, 14)}[fmt]
    v = np.moveaxis(np.asarray(x, np.float32).astype(ml_dtypes.bfloat16).astype(np.float64), axis, -1)
    blocks = v.reshape(v.shape[:-1] + (-1, 32))
    amax = np.abs(blocks).max(-1, keepdims=True)
    byte = np.maximum(np.where(amax > 0, np.frexp(amax)[1] - 1 + 127, 0) - down, 1)
    scale = np.exp2(byte - 127.0)
    codes = (blocks / scale).astype(np.float32).astype(dtype).astype(np.float64)
    return np.moveaxis((codes * scale).reshape(v.shape), -1, axis)


WIDE = False


def mx_kscale(k):
    if not WIDE:
        return np.ones(k)
    levels = np.array([10, -10, 5, -5, 0])
    a = np.random.permutation(np.resize(levels, k // 512 * 4)).reshape(k // 512, 4)
    idx = np.arange(k)
    return np.exp2(a[idx // 512, idx % 128 // 32])


BF16 = ml_dtypes.bfloat16


def bf(x):
    return np.asarray(x, np.float32).astype(BF16)


def f64(x):
    return np.asarray(x).astype(np.float64)


E2M1 = np.array([0.0, 0.5, 1.0, 1.5, 2.0, 3.0, 4.0, 6.0, -0.0, -0.5, -1.0, -1.5, -2.0, -3.0, -4.0, -6.0])


def pack_weight(w, fmt):
    k, n = w.shape
    w = f64(bf(w)).reshape(k // 32, 32, n)
    amax = np.abs(w).max(1)
    if fmt == "e4m3":
        byte = np.frexp(amax)[1] - 1 + 127 - 7
    else:
        mant, ex = np.frexp(amax / 6.0)
        byte = np.where(mant > 0.5, ex, ex - 1) + 127
    byte = np.clip(np.where(amax > 0, byte, 1), 1, 254)
    scaled = (w * np.exp2(127.0 - byte)[:, None, :]).reshape(k, n).astype(np.float32)
    by_word = np.ascontiguousarray(scaled.reshape(k // 512, 128, 4, n).transpose(0, 1, 3, 2))
    if fmt == "e4m3":
        words = by_word.astype(ml_dtypes.float8_e4m3fn).view(np.uint8)
    else:
        c = by_word.astype(ml_dtypes.float4_e2m1fn).view(np.uint8) & 0xF
        words = c[..., 0::2] | (c[..., 1::2] << 4)
    return np.ascontiguousarray(words), np.ascontiguousarray(byte.astype(np.uint8).reshape(k // 512, 16, n))


def unpack_weight(words, scales, fmt):
    g, p, n, _ = words.shape
    if fmt == "e4m3":
        vals = np.ascontiguousarray(words).view(ml_dtypes.float8_e4m3fn).astype(np.float64)
    else:
        nib = np.empty((g, p, n, 4), np.uint8)
        nib[..., 0::2] = words & 0xF
        nib[..., 1::2] = words >> 4
        vals = E2M1[nib]
    vals = vals * np.repeat(np.exp2(scales.astype(np.float64) - 127.0), 8, axis=1)[..., None]
    return vals.transpose(0, 1, 3, 2).reshape(g * 512, n)


NQ, NK, QS, KS, F, DEG = 4096, 1024, 1024, 512, 512, 32
EPS = 1e-5
SLOPE = 0.01
FMT = "e4m3"


def leaky(v):
    return np.where(v >= 0, v, SLOPE * v)


def setup_inputs():
    s, t = mx_kscale(QS), mx_kscale(F)
    x = bf(np.random.standard_normal((NQ, QS)) * s)
    w1_words, w1_scales = pack_weight(np.random.standard_normal((QS, F)) / np.sqrt(QS) / s[:, None] * t, FMT)
    b1 = bf(np.random.standard_normal(F) * 0.5 * t)
    w2_words, w2_scales = pack_weight(np.random.standard_normal((F, F)) / np.sqrt(F) / t[:, None], FMT)
    b2 = bf(np.random.standard_normal(F) * 0.5)
    gamma = bf(1.0 + 0.1 * np.random.standard_normal(F))
    beta = bf(0.1 * np.random.standard_normal(F))
    return {"x": x,
            "w1_words": w1_words,
            "w1_scales": w1_scales,
            "b1": b1,
            "w2_words": w2_words,
            "w2_scales": w2_scales,
            "b2": b2,
            "gamma": gamma,
            "beta": beta}


def reference(x, w1_words, w1_scales, b1, w2_words, w2_scales, b2, gamma, beta):
    h = leaky((mxq(f64(x), 1, "e4m3") @ unpack_weight(w1_words, w1_scales, FMT)) + f64(b1))
    h = leaky((mxq(h, 1, "e4m3") @ unpack_weight(w2_words, w2_scales, FMT)) + f64(b2))
    mean = h.mean(axis=0)
    var = h.var(axis=0)
    return f64(gamma) * (h - mean) / np.sqrt(var + EPS) + f64(beta)

@@ -1,0 +1,307 @@
+from contextlib import ExitStack
+
+import concourse.mybir as mybir
+from concourse.masks import make_identity
+
+F32 = mybir.dt.float32
+BF16 = mybir.dt.bfloat16
+I32 = mybir.dt.int32
+U32 = mybir.dt.uint32
+U8 = mybir.dt.uint8
+FP8X4 = mybir.dt.float8_e4m3fn_x4
+ALU = mybir.AluOpType
+ACT = mybir.ActivationFunctionType
+
+P = 128
+ROWS = 4096
+K1 = 1024
+F = 512
+K_PASS = 512
+PASSES1 = K1 // K_PASS
+PAIR_ROWS = 2 * P
+GROUP_ROWS = 4 * P
+PAIRS = ROWS // PAIR_ROWS
+GROUPS = ROWS // GROUP_ROWS
+F_BLOCKS = F // P
+SLOPE = 0.01
+EPS = 1e-5
+
+FLOPS = 2 * ROWS * K1 * F + 2 * ROWS * F * F
+
+
+def tile_attention_prop_pa_t_kernel(
+    tc, x, w1_words, w1_scales, b1, w2_words, w2_scales, b2, gamma, beta, out
+):
+    nc = tc.nc
+    with ExitStack() as stack:
+        keep = stack.enter_context(tc.tile_pool(name="keep", bufs=1))
+        x_pool = stack.enter_context(tc.tile_pool(name="x_pool", bufs=6))
+        quant = stack.enter_context(tc.tile_pool(name="quant", bufs=3))
+        work = stack.enter_context(tc.tile_pool(name="work", bufs=4))
+
+        one = keep.tile([P, 1], F32)
+        nc.vector.memset(one[:], 1.0)
+        warm = keep.tile([P, 1], F32)
+        nc.scalar.activation(out=warm[:], in_=one[:], func=ACT.Sqrt)
+
+        planes = keep.tile([P, PASSES1 + 1, F], U8, align_bytes=64)
+        nc.vector.memset(planes[:].bitcast(I32), 0)
+        for q in range(4):
+            nc.sync.dma_start(
+                out=planes[32 * q : 32 * q + 4, 0:PASSES1, :].bitcast(I32),
+                in_=w1_scales[:, 4 * q : 4 * q + 4, :].rearrange("g r n -> r g n").bitcast(I32),
+            )
+            nc.sync.dma_start(
+                out=planes[32 * q : 32 * q + 4, PASSES1, :].bitcast(I32),
+                in_=w2_scales[0, 4 * q : 4 * q + 4, :].bitcast(I32),
+            )
+
+        x_tiles = []
+
+        def load_x(group):
+            x_sb = x_pool.tile([P, 4, K1], BF16, name="x_sb")
+            rows = x[group * GROUP_ROWS : (group + 1) * GROUP_ROWS, :]
+            nc.sync.dma_start(out=x_sb[:], in_=rows.rearrange("(p j) k -> p j k", j=4))
+            x_tiles.append(x_sb)
+
+        load_x(0)
+        w1_sb = keep.tile([P, PASSES1, F], U32, align_bytes=64)
+        nc.sync.dma_start(
+            out=w1_sb[:].bitcast(I32),
+            in_=w1_words.rearrange("g p n t -> p g (n t)").bitcast(I32),
+        )
+        b1_row = keep.tile([P, F], BF16)
+        nc.vector.memset(b1_row[:], 0.0)
+        nc.sync.dma_start(out=b1_row[0:1, :], in_=b1.rearrange("(o n) -> o n", o=1))
+        vec_rows = keep.tile([P, P], BF16)
+        nc.vector.memset(vec_rows[:], 0.0)
+        for i, vec in enumerate((b2, gamma, beta)):
+            nc.sync.dma_start(
+                out=vec_rows[F_BLOCKS * i : F_BLOCKS * (i + 1), :],
+                in_=vec.rearrange("(f c) -> f c", c=P),
+            )
+        w2_sb = keep.tile([P, F], U32, align_bytes=64)
+        nc.sync.dma_start(
+            out=w2_sb[:].bitcast(I32),
+            in_=w2_words[0].rearrange("p n t -> p (n t)").bitcast(I32),
+        )
+        for group in range(1, GROUPS):
+            load_x(group)
+
+        ident_f32 = keep.tile([P, P], F32)
+        make_identity(nc, ident_f32[:])
+        ident_bf16 = keep.tile([P, P], BF16)
+        make_identity(nc, ident_bf16[:])
+        ones = keep.tile([P, P], BF16)
+        nc.vector.memset(ones[:], 1.0)
+
+        h2t = keep.tile([P, F_BLOCKS, ROWS], F32)
+        sums = keep.tile([P, F_BLOCKS, GROUPS], F32)
+        squares = keep.tile([P, F_BLOCKS, GROUPS], F32)
+        b1_all = keep.tile([P, 2, P, 2], F32)
+        vec_cols = keep.tile([P, 3 * F_BLOCKS], F32)
+        b2_slope = keep.tile([P, F_BLOCKS], F32)
+
+        with ExitStack() as main:
+            ps_setup = main.enter_context(tc.psum_pool(name="ps_setup", bufs=1))
+            ps_xt = main.enter_context(tc.psum_pool(name="ps_xt", bufs=2))
+            ps_acc1 = main.enter_context(tc.psum_pool(name="ps_acc1", bufs=2))
+            ps_ht = main.enter_context(tc.psum_pool(name="ps_ht", bufs=1))
+            ps_acc2 = main.enter_context(tc.psum_pool(name="ps_acc2", bufs=2))
+
+            b1_ps = ps_setup.tile([P, F], F32, tag="setup")
+            nc.tensor.matmul(out=b1_ps[:], lhsT=ones[:], rhs=b1_row[:], start=True, stop=True)
+            nc.vector.tensor_copy(
+                out=b1_all[:], in_=b1_ps[:].rearrange("p (c u e) -> p u c e", u=2, e=2)
+            )
+            vec_ps = ps_setup.tile([P, P], BF16, tag="setup")
+            nc.tensor.transpose(vec_ps[:], vec_rows[:], ident_bf16[:])
+            nc.vector.tensor_copy(out=vec_cols[:], in_=vec_ps[:, 0 : 3 * F_BLOCKS])
+            nc.vector.tensor_scalar_mul(
+                out=b2_slope[:], in0=vec_cols[:, 0:F_BLOCKS], scalar1=SLOPE
+            )
+
+            x_codes = {}
+            h1_tiles = {}
+            h1_grouped = {}
+
+            def quantise_x(pair):
+                x_words = x_tiles[pair // 2][:].bitcast(F32)
+                grouped = quant.tile([P, PASSES1, PAIR_ROWS, 4], BF16, name="x_grouped", align_bytes=64)
+                for g in range(PASSES1):
+                    xt = ps_xt.tile([P, 2, PAIR_ROWS], F32, name="xt")
+                    for jj in range(2):
+                        j = 2 * (pair % 2) + jj
+                        for u in range(2):
+                            nc.tensor.transpose(
+                                xt[:, u, jj * P : (jj + 1) * P],
+                                x_words[:, j, 256 * g + u : 256 * (g + 1) : 2],
+                                ident_f32[:],
+                            )
+                    nc.scalar.copy(
+                        out=grouped[:, g].bitcast(F32), in_=xt[:].rearrange("p u r -> p r u")
+                    )
+                codes = quant.tile([P, PASSES1, PAIR_ROWS], U32, name="x_code", align_bytes=64)
+                scales = quant.tile([P, PASSES1, PAIR_ROWS], U8, name="x_scale", align_bytes=64)
+                nc.vector.quantize_mx(
+                    out=codes[:].rearrange("p g r -> p (g r)").bitcast(FP8X4),
+                    scales=scales[:].rearrange("p g r -> p (g r)"),
+                    in_=grouped[:].rearrange("p g r t -> p (g r t)"),
+                )
+                x_codes[pair] = (codes, scales)
+
+            def layer1(pair):
+                codes, scales = x_codes.pop(pair)
+                for jj in range(2):
+                    rows = slice(jj * P, (jj + 1) * P)
+                    acc1 = ps_acc1.tile([P, F], F32, name="acc1")
+                    for g in range(PASSES1):
+                        nc.tensor.matmul_mx(
+                            out=acc1[:],
+                            lhsT=codes[:, g, rows].bitcast(FP8X4),
+                            lhsT_scale=scales[:, g, rows],
+                            rhs=w1_sb[:, g, :].bitcast(FP8X4),
+                            rhs_scale=planes[:, g, :],
+                            start=(g == 0),
+                            stop=(g == PASSES1 - 1),
+                        )
+                    v = work.tile([P, 2, P, 2], F32, name="v")
+                    nc.vector.tensor_tensor(
+                        out=v[:],
+                        in0=acc1[:].rearrange("p (c u e) -> p u c e", u=2, e=2),
+                        in1=b1_all[:],
+                        op=ALU.add,
+                    )
+                    v_flat = v[:].rearrange("p u c e -> p (u c e)")
+                    h1 = work.tile([P, F], BF16, name="h1")
+                    nc.vector.scalar_tensor_tensor(
+                        out=h1[:], in0=v_flat, scalar=SLOPE, in1=v_flat, op0=ALU.mult, op1=ALU.max
+                    )
+                    h1_tiles[(pair, jj)] = h1
+
+            def transpose_h1(pair):
+                if pair % 2 == 0:
+                    h1_grouped[pair // 2] = quant.tile(
+                        [P, GROUP_ROWS, 4], BF16, name="h_grouped", align_bytes=64
+                    )
+                grouped = h1_grouped[pair // 2]
+                ht = ps_ht.tile([P, 2, PAIR_ROWS], F32, name="ht")
+                for jj in range(2):
+                    h1_words = h1_tiles.pop((pair, jj))[:].bitcast(F32)
+                    for u in range(2):
+                        nc.tensor.transpose(
+                            ht[:, u, jj * P : (jj + 1) * P],
+                            h1_words[:, u * P : (u + 1) * P],
+                            ident_f32[:],
+                        )
+                first = (pair % 2) * PAIR_ROWS
+                nc.scalar.copy(
+                    out=grouped[:, first : first + PAIR_ROWS, :].bitcast(F32),
+                    in_=ht[:].rearrange("p u r -> p r u"),
+                )
+
+            def layer2(group):
+                grouped = h1_grouped.pop(group)
+                codes = quant.tile([P, GROUP_ROWS], U32, name="h_code", align_bytes=64)
+                scales = quant.tile([P, GROUP_ROWS], U8, name="h_scale", align_bytes=64)
+                nc.vector.quantize_mx(
+                    out=codes[:].bitcast(FP8X4),
+                    scales=scales[:],
+                    in_=grouped[:].rearrange("p r t -> p (r t)"),
+                )
+                cols = slice(group * GROUP_ROWS, (group + 1) * GROUP_ROWS)
+                for fb in range(F_BLOCKS):
+                    feats = slice(fb * P, (fb + 1) * P)
+                    acc2 = ps_acc2.tile([P, GROUP_ROWS], F32, name="acc2")
+                    nc.tensor.matmul_mx(
+                        out=acc2[:],
+                        lhsT=w2_sb[:, feats].bitcast(FP8X4),
+                        lhsT_scale=planes[:, PASSES1, feats],
+                        rhs=codes[:].bitcast(FP8X4),
+                        rhs_scale=scales[:],
+                        start=True,
+                        stop=True,
+                    )
+                    low = work.tile([P, GROUP_ROWS], F32, name="low")
+                    nc.scalar.activation(
+                        out=low[:],
+                        in_=acc2[:],
+                        func=ACT.Identity,
+                        scale=SLOPE,
+                        bias=b2_slope[:, fb : fb + 1],
+                    )
+                    nc.vector.scalar_tensor_tensor(
+                        out=h2t[:, fb, cols],
+                        in0=acc2[:],
+                        scalar=vec_cols[:, fb : fb + 1],
+                        in1=low[:],
+                        op0=ALU.add,
+                        op1=ALU.max,
+                        accum_out=sums[:, fb, group : group + 1],
+                    )
+                    unread = work.tile([P, GROUP_ROWS], BF16, name="unread")
+                    nc.scalar.activation(
+                        out=unread[:],
+                        in_=h2t[:, fb, cols],
+                        func=ACT.Square,
+                        accum_out=squares[:, fb, group : group + 1],
+                    )
+
+            for step in range(PAIRS + 3):
+                if step < PAIRS:
+                    quantise_x(step)
+                if 0 <= step - 1 < PAIRS:
+                    layer1(step - 1)
+                if 0 <= step - 2 < PAIRS:
+                    transpose_h1(step - 2)
+                if 0 <= step - 3 < PAIRS and (step - 3) % 2 == 1:
+                    layer2((step - 3) // 2)
+
+        mean = keep.tile([P, F_BLOCKS], F32)
+        nc.vector.tensor_reduce(out=mean[:], in_=sums[:], axis=mybir.AxisListType.X, op=ALU.add)
+        nc.vector.tensor_scalar_mul(out=mean[:], in0=mean[:], scalar1=1.0 / ROWS)
+        var = keep.tile([P, F_BLOCKS], F32)
+        nc.vector.tensor_reduce(out=var[:], in_=squares[:], axis=mybir.AxisListType.X, op=ALU.add)
+        mean_sq = keep.tile([P, F_BLOCKS], F32)
+        nc.vector.tensor_mul(out=mean_sq[:], in0=mean[:], in1=mean[:])
+        nc.vector.scalar_tensor_tensor(
+            out=var[:], in0=var[:], scalar=1.0 / ROWS, in1=mean_sq[:], op0=ALU.mult, op1=ALU.subtract
+        )
+        nc.vector.tensor_scalar_add(out=var[:], in0=var[:], scalar1=EPS)
+        std = keep.tile([P, F_BLOCKS], F32)
+        nc.scalar.activation(out=std[:], in_=var[:], func=ACT.Sqrt)
+        gain = keep.tile([P, F_BLOCKS], F32)
+        nc.vector.reciprocal(out=gain[:], in_=std[:])
+        nc.vector.tensor_mul(out=gain[:], in0=gain[:], in1=vec_cols[:, F_BLOCKS : 2 * F_BLOCKS])
+        shift = keep.tile([P, F_BLOCKS], F32)
+        nc.vector.tensor_mul(out=shift[:], in0=mean[:], in1=gain[:])
+        nc.vector.tensor_sub(out=shift[:], in0=vec_cols[:, 2 * F_BLOCKS : 3 * F_BLOCKS], in1=shift[:])
+
+        with ExitStack() as tail:
+            ps_out = tail.enter_context(tc.psum_pool(name="ps_out", bufs=4))
+            stage_pool = tail.enter_context(tc.tile_pool(name="stage_pool", bufs=3))
+            for group in range(GROUPS):
+                cols = slice(group * GROUP_ROWS, (group + 1) * GROUP_ROWS)
+                for fb in range(F_BLOCKS):
+                    nc.vector.tensor_scalar(
+                        out=h2t[:, fb, cols],
+                        in0=h2t[:, fb, cols],
+                        scalar1=gain[:, fb : fb + 1],
+                        scalar2=shift[:, fb : fb + 1],
+                        op0=ALU.mult,
+                        op1=ALU.add,
+                    )
+                stage = stage_pool.tile([P, 4, F], F32, name="stage")
+                for j in range(4):
+                    first = group * GROUP_ROWS + j * P
+                    ot = ps_out.tile([P, F], F32, name="ot")
+                    for fb in range(F_BLOCKS):
+                        nc.tensor.transpose(
+                            ot[:, fb * P : (fb + 1) * P], h2t[:, fb, first : first + P], ident_f32[:]
+                        )
+                    if j == 3:
+                        nc.vector.tensor_copy(out=stage[:, j, :], in_=ot[:])
+                    else:
+                        nc.scalar.copy(out=stage[:, j, :], in_=ot[:])
+                rows = out[group * GROUP_ROWS : (group + 1) * GROUP_ROWS, :]
+                nc.sync.dma_start(out=rows.rearrange("(p j) f -> p j f", j=4), in_=stage[:])

@@ -18,9 +18,9 @@ K1 = 1024
 F = 512
 K_PASS = 512
 PASSES1 = K1 // K_PASS
-PAIR_ROWS = 2 * P
+PACK = 4
 GROUP_ROWS = 4 * P
-PAIRS = ROWS // PAIR_ROWS
+HALF_ROWS = 2 * P
 GROUPS = ROWS // GROUP_ROWS
 F_BLOCKS = F // P
 SLOPE = 0.01
@@ -35,9 +35,6 @@ def tile_attention_prop_pa_t_kernel(
     nc = tc.nc
     with ExitStack() as stack:
         keep = stack.enter_context(tc.tile_pool(name="keep", bufs=1))
-        x_pool = stack.enter_context(tc.tile_pool(name="x_pool", bufs=6))
-        quant = stack.enter_context(tc.tile_pool(name="quant", bufs=3))
-        work = stack.enter_context(tc.tile_pool(name="work", bufs=4))
 
         one = keep.tile([P, 1], F32)
         nc.vector.memset(one[:], 1.0)
@@ -56,154 +53,151 @@ def tile_attention_prop_pa_t_kernel(
                 in_=w2_scales[0, 4 * q : 4 * q + 4, :].bitcast(I32),
             )
 
-        x_tiles = []
-
-        def load_x(group):
-            x_sb = x_pool.tile([P, 4, K1], BF16, name="x_sb")
-            rows = x[group * GROUP_ROWS : (group + 1) * GROUP_ROWS, :]
-            nc.sync.dma_start(out=x_sb[:], in_=rows.rearrange("(p j) k -> p j k", j=4))
-            x_tiles.append(x_sb)
-
-        load_x(0)
-        w1_sb = keep.tile([P, PASSES1, F], U32, align_bytes=64)
-        nc.sync.dma_start(
-            out=w1_sb[:].bitcast(I32),
-            in_=w1_words.rearrange("g p n t -> p g (n t)").bitcast(I32),
-        )
-        b1_row = keep.tile([P, F], BF16)
-        nc.vector.memset(b1_row[:], 0.0)
-        nc.sync.dma_start(out=b1_row[0:1, :], in_=b1.rearrange("(o n) -> o n", o=1))
-        vec_rows = keep.tile([P, P], BF16)
-        nc.vector.memset(vec_rows[:], 0.0)
-        for i, vec in enumerate((b2, gamma, beta)):
-            nc.sync.dma_start(
-                out=vec_rows[F_BLOCKS * i : F_BLOCKS * (i + 1), :],
-                in_=vec.rearrange("(f c) -> f c", c=P),
-            )
-        w2_sb = keep.tile([P, F], U32, align_bytes=64)
-        nc.sync.dma_start(
-            out=w2_sb[:].bitcast(I32),
-            in_=w2_words[0].rearrange("p n t -> p (n t)").bitcast(I32),
-        )
-        for group in range(1, GROUPS):
-            load_x(group)
-
-        ident_f32 = keep.tile([P, P], F32)
-        make_identity(nc, ident_f32[:])
-        ident_bf16 = keep.tile([P, P], BF16)
-        make_identity(nc, ident_bf16[:])
-        ones = keep.tile([P, P], BF16)
-        nc.vector.memset(ones[:], 1.0)
-
-        h2t = keep.tile([P, F_BLOCKS, ROWS], F32)
-        sums = keep.tile([P, F_BLOCKS, GROUPS], F32)
-        squares = keep.tile([P, F_BLOCKS, GROUPS], F32)
-        b1_all = keep.tile([P, 2, P, 2], F32)
-        vec_cols = keep.tile([P, 3 * F_BLOCKS], F32)
-        b2_slope = keep.tile([P, F_BLOCKS], F32)
-
         with ExitStack() as main:
-            ps_setup = main.enter_context(tc.psum_pool(name="ps_setup", bufs=1))
-            ps_xt = main.enter_context(tc.psum_pool(name="ps_xt", bufs=2))
-            ps_acc1 = main.enter_context(tc.psum_pool(name="ps_acc1", bufs=2))
-            ps_ht = main.enter_context(tc.psum_pool(name="ps_ht", bufs=1))
-            ps_acc2 = main.enter_context(tc.psum_pool(name="ps_acc2", bufs=2))
+            x_pool = main.enter_context(tc.tile_pool(name="x_pool", bufs=6))
+            x_tiles = []
 
-            b1_ps = ps_setup.tile([P, F], F32, tag="setup")
-            nc.tensor.matmul(out=b1_ps[:], lhsT=ones[:], rhs=b1_row[:], start=True, stop=True)
-            nc.vector.tensor_copy(
-                out=b1_all[:], in_=b1_ps[:].rearrange("p (c u e) -> p u c e", u=2, e=2)
+            def load_x(group):
+                x_sb = x_pool.tile([P, 4, K1], BF16, name="x_sb")
+                rows = x[group * GROUP_ROWS : (group + 1) * GROUP_ROWS, :]
+                nc.sync.dma_start(out=x_sb[:], in_=rows.rearrange("(p j) k -> p j k", j=4))
+                x_tiles.append(x_sb)
+
+            load_x(0)
+            w1_raw = keep.tile([P, PASSES1, F], U32)
+            nc.sync.dma_start(
+                out=w1_raw[:].bitcast(I32),
+                in_=w1_words.rearrange("g p n t -> p g (n t)").bitcast(I32),
             )
-            vec_ps = ps_setup.tile([P, P], BF16, tag="setup")
-            nc.tensor.transpose(vec_ps[:], vec_rows[:], ident_bf16[:])
-            nc.vector.tensor_copy(out=vec_cols[:], in_=vec_ps[:, 0 : 3 * F_BLOCKS])
-            nc.vector.tensor_scalar_mul(
-                out=b2_slope[:], in0=vec_cols[:, 0:F_BLOCKS], scalar1=SLOPE
-            )
-
-            x_codes = {}
-            h1_tiles = {}
-            h1_grouped = {}
-
-            def quantise_x(pair):
-                x_words = x_tiles[pair // 2][:].bitcast(F32)
-                grouped = quant.tile([P, PASSES1, PAIR_ROWS, 4], BF16, name="x_grouped", align_bytes=64)
-                for g in range(PASSES1):
-                    xt = ps_xt.tile([P, 2, PAIR_ROWS], F32, name="xt")
-                    for jj in range(2):
-                        j = 2 * (pair % 2) + jj
-                        for u in range(2):
-                            nc.tensor.transpose(
-                                xt[:, u, jj * P : (jj + 1) * P],
-                                x_words[:, j, 256 * g + u : 256 * (g + 1) : 2],
-                                ident_f32[:],
-                            )
-                    nc.scalar.copy(
-                        out=grouped[:, g].bitcast(F32), in_=xt[:].rearrange("p u r -> p r u")
-                    )
-                codes = quant.tile([P, PASSES1, PAIR_ROWS], U32, name="x_code", align_bytes=64)
-                scales = quant.tile([P, PASSES1, PAIR_ROWS], U8, name="x_scale", align_bytes=64)
-                nc.vector.quantize_mx(
-                    out=codes[:].rearrange("p g r -> p (g r)").bitcast(FP8X4),
-                    scales=scales[:].rearrange("p g r -> p (g r)"),
-                    in_=grouped[:].rearrange("p g r t -> p (g r t)"),
+            b1_bf = keep.tile([P, PACK], BF16)
+            nc.sync.dma_start(out=b1_bf[:], in_=b1.rearrange("(p t) -> p t", t=PACK))
+            vec_rows = keep.tile([P, P], BF16)
+            nc.vector.memset(vec_rows[:], 0.0)
+            for i, vec in enumerate((b2, gamma, beta)):
+                nc.sync.dma_start(
+                    out=vec_rows[F_BLOCKS * i : F_BLOCKS * (i + 1), :],
+                    in_=vec.rearrange("(f c) -> f c", c=P),
                 )
-                x_codes[pair] = (codes, scales)
+            w2_sb = keep.tile([P, F], U32, align_bytes=64)
+            nc.sync.dma_start(
+                out=w2_sb[:].bitcast(I32),
+                in_=w2_words[0].rearrange("p n t -> p (n t)").bitcast(I32),
+            )
+            for group in range(1, GROUPS):
+                load_x(group)
 
-            def layer1(pair):
-                codes, scales = x_codes.pop(pair)
-                for jj in range(2):
-                    rows = slice(jj * P, (jj + 1) * P)
-                    acc1 = ps_acc1.tile([P, F], F32, name="acc1")
+            ident_f32 = keep.tile([P, P], F32)
+            make_identity(nc, ident_f32[:])
+            ident_bf16 = keep.tile([P, P], BF16)
+            make_identity(nc, ident_bf16[:])
+
+            planes1 = keep.tile([P, PASSES1, F], U8, align_bytes=64)
+            nc.vector.tensor_copy(
+                out=planes1[:].rearrange("p g (t m) -> p g m t", t=PACK),
+                in_=planes[:, 0:PASSES1, :].rearrange("p g (m t) -> p g m t", t=PACK),
+            )
+            w1_sb = keep.tile([P, PASSES1, F], U32, align_bytes=64)
+            nc.vector.tensor_copy(
+                out=w1_sb[:].bitcast(I32).rearrange("p g (t m) -> p g t m", t=PACK),
+                in_=w1_raw[:].bitcast(I32).rearrange("p g (m t) -> p g t m", t=PACK),
+            )
+            b1_cols = keep.tile([P, PACK], F32)
+            nc.vector.tensor_copy(out=b1_cols[:], in_=b1_bf[:])
+
+            h2t = keep.tile([P, F_BLOCKS, ROWS], F32)
+            sums = keep.tile([P, F_BLOCKS, GROUPS], F32)
+            squares = keep.tile([P, F_BLOCKS, GROUPS], F32)
+            vec_cols = keep.tile([P, 3 * F_BLOCKS], F32)
+            b2_slope = keep.tile([P, F_BLOCKS], F32)
+
+            with tc.psum_pool(name="ps_setup", bufs=1) as ps_setup:
+                vec_ps = ps_setup.tile([P, P], BF16, name="vec_ps")
+                nc.tensor.transpose(vec_ps[:], vec_rows[:], ident_bf16[:])
+                nc.vector.tensor_copy(out=vec_cols[:], in_=vec_ps[:, 0 : 3 * F_BLOCKS])
+            nc.vector.tensor_scalar_mul(out=b2_slope[:], in0=vec_cols[:, 0:F_BLOCKS], scalar1=SLOPE)
+
+            xq = main.enter_context(tc.tile_pool(name="xq", bufs=4))
+            hq = main.enter_context(tc.tile_pool(name="hq", bufs=3))
+            v_pool = main.enter_context(tc.tile_pool(name="v_pool", bufs=3))
+            work = main.enter_context(tc.tile_pool(name="work", bufs=4))
+            ps_xt = main.enter_context(tc.psum_pool(name="ps_xt", bufs=2))
+            ps_acc1 = main.enter_context(tc.psum_pool(name="ps_acc1", bufs=3))
+            ps_acc2 = main.enter_context(tc.psum_pool(name="ps_acc2", bufs=3))
+
+            x_grouped = {}
+            x_codes = {}
+            v_tiles = {}
+            h_grouped = {}
+
+            def transpose_x(group):
+                x_words = x_tiles[group][:].bitcast(F32)
+                for g in range(PASSES1):
+                    grouped = xq.tile([P, GROUP_ROWS, PACK], BF16, name="x_grouped", align_bytes=64)
+                    for half in range(2):
+                        xt = ps_xt.tile([P, 2, HALF_ROWS], F32, name="xt")
+                        for jj in range(2):
+                            j = 2 * half + jj
+                            for u in range(2):
+                                nc.tensor.transpose(
+                                    xt[:, u, jj * P : (jj + 1) * P],
+                                    x_words[:, j, 256 * g + u : 256 * (g + 1) : 2],
+                                    ident_f32[:],
+                                )
+                        dst = grouped[:, half * HALF_ROWS : (half + 1) * HALF_ROWS, :].bitcast(F32)
+                        src = xt[:].rearrange("p u r -> p r u")
+                        if half == 0:
+                            nc.scalar.copy(out=dst, in_=src)
+                        else:
+                            nc.vector.tensor_copy(out=dst, in_=src)
+                    x_grouped[(group, g)] = grouped
+
+            def quantise_x(group):
+                for g in range(PASSES1):
+                    grouped = x_grouped.pop((group, g))
+                    codes = xq.tile([P, GROUP_ROWS], U32, name="x_code", align_bytes=64)
+                    scales = xq.tile([P, GROUP_ROWS], U8, name="x_scale", align_bytes=64)
+                    nc.vector.quantize_mx(
+                        out=codes[:].bitcast(FP8X4),
+                        scales=scales[:],
+                        in_=grouped[:].rearrange("p r t -> p (r t)"),
+                    )
+                    x_codes[(group, g)] = (codes, scales)
+
+            def layer1(group):
+                v = v_pool.tile([P, PACK, GROUP_ROWS], F32, name="v")
+                for t in range(PACK):
+                    feats = slice(t * P, (t + 1) * P)
+                    acc1 = ps_acc1.tile([P, GROUP_ROWS], F32, name="acc1")
                     for g in range(PASSES1):
+                        codes, scales = x_codes[(group, g)]
                         nc.tensor.matmul_mx(
                             out=acc1[:],
-                            lhsT=codes[:, g, rows].bitcast(FP8X4),
-                            lhsT_scale=scales[:, g, rows],
-                            rhs=w1_sb[:, g, :].bitcast(FP8X4),
-                            rhs_scale=planes[:, g, :],
+                            lhsT=w1_sb[:, g, feats].bitcast(FP8X4),
+                            lhsT_scale=planes1[:, g, feats],
+                            rhs=codes[:].bitcast(FP8X4),
+                            rhs_scale=scales[:],
                             start=(g == 0),
                             stop=(g == PASSES1 - 1),
                         )
-                    v = work.tile([P, 2, P, 2], F32, name="v")
-                    nc.vector.tensor_tensor(
-                        out=v[:],
-                        in0=acc1[:].rearrange("p (c u e) -> p u c e", u=2, e=2),
-                        in1=b1_all[:],
-                        op=ALU.add,
+                    nc.scalar.activation(
+                        out=v[:, t, :], in_=acc1[:], func=ACT.Identity, bias=b1_cols[:, t : t + 1]
                     )
-                    v_flat = v[:].rearrange("p u c e -> p (u c e)")
-                    h1 = work.tile([P, F], BF16, name="h1")
-                    nc.vector.scalar_tensor_tensor(
-                        out=h1[:], in0=v_flat, scalar=SLOPE, in1=v_flat, op0=ALU.mult, op1=ALU.max
-                    )
-                    h1_tiles[(pair, jj)] = h1
+                for g in range(PASSES1):
+                    x_codes.pop((group, g))
+                v_tiles[group] = v
 
-            def transpose_h1(pair):
-                if pair % 2 == 0:
-                    h1_grouped[pair // 2] = quant.tile(
-                        [P, GROUP_ROWS, 4], BF16, name="h_grouped", align_bytes=64
-                    )
-                grouped = h1_grouped[pair // 2]
-                ht = ps_ht.tile([P, 2, PAIR_ROWS], F32, name="ht")
-                for jj in range(2):
-                    h1_words = h1_tiles.pop((pair, jj))[:].bitcast(F32)
-                    for u in range(2):
-                        nc.tensor.transpose(
-                            ht[:, u, jj * P : (jj + 1) * P],
-                            h1_words[:, u * P : (u + 1) * P],
-                            ident_f32[:],
-                        )
-                first = (pair % 2) * PAIR_ROWS
-                nc.scalar.copy(
-                    out=grouped[:, first : first + PAIR_ROWS, :].bitcast(F32),
-                    in_=ht[:].rearrange("p u r -> p r u"),
+            def leaky1(group):
+                v_rt = v_tiles.pop(group)[:].rearrange("p t r -> p r t")
+                grouped = hq.tile([P, GROUP_ROWS, PACK], BF16, name="h_grouped", align_bytes=64)
+                nc.vector.scalar_tensor_tensor(
+                    out=grouped[:], in0=v_rt, scalar=SLOPE, in1=v_rt, op0=ALU.mult, op1=ALU.max
                 )
+                h_grouped[group] = grouped
 
             def layer2(group):
-                grouped = h1_grouped.pop(group)
-                codes = quant.tile([P, GROUP_ROWS], U32, name="h_code", align_bytes=64)
-                scales = quant.tile([P, GROUP_ROWS], U8, name="h_scale", align_bytes=64)
+                grouped = h_grouped.pop(group)
+                codes = hq.tile([P, GROUP_ROWS], U32, name="h_code", align_bytes=64)
+                scales = hq.tile([P, GROUP_ROWS], U8, name="h_scale", align_bytes=64)
                 nc.vector.quantize_mx(
                     out=codes[:].bitcast(FP8X4),
                     scales=scales[:],
@@ -247,15 +241,16 @@ def tile_attention_prop_pa_t_kernel(
                         accum_out=squares[:, fb, group : group + 1],
                     )
 
-            for step in range(PAIRS + 3):
-                if step < PAIRS:
-                    quantise_x(step)
-                if 0 <= step - 1 < PAIRS:
+            for step in range(GROUPS + 3):
+                if step < GROUPS:
+                    transpose_x(step)
+                if 0 <= step - 1 < GROUPS:
+                    quantise_x(step - 1)
                     layer1(step - 1)
-                if 0 <= step - 2 < PAIRS:
-                    transpose_h1(step - 2)
-                if 0 <= step - 3 < PAIRS and (step - 3) % 2 == 1:
-                    layer2((step - 3) // 2)
+                if 0 <= step - 2 < GROUPS:
+                    leaky1(step - 2)
+                if 0 <= step - 3 < GROUPS:
+                    layer2(step - 3)
 
         mean = keep.tile([P, F_BLOCKS], F32)
         nc.vector.tensor_reduce(out=mean[:], in_=sums[:], axis=mybir.AxisListType.X, op=ALU.add)

@@ -35,6 +35,15 @@ def tile_attention_prop_pa_t_kernel(
     nc = tc.nc
     with ExitStack() as stack:
         keep = stack.enter_context(tc.tile_pool(name="keep", bufs=1))
+        x_pool = stack.enter_context(tc.tile_pool(name="x_pool", bufs=6))
+        xg_pool = stack.enter_context(tc.tile_pool(name="xg_pool", bufs=4))
+        xc_pool = stack.enter_context(tc.tile_pool(name="xc_pool", bufs=6))
+        v_pool = stack.enter_context(tc.tile_pool(name="v_pool", bufs=3))
+        hg_pool = stack.enter_context(tc.tile_pool(name="hg_pool", bufs=2))
+        work = stack.enter_context(tc.tile_pool(name="work", bufs=4))
+        ps_xt = stack.enter_context(tc.psum_pool(name="ps_xt", bufs=2))
+        ps_acc1 = stack.enter_context(tc.psum_pool(name="ps_acc1", bufs=3))
+        ps_acc2 = stack.enter_context(tc.psum_pool(name="ps_acc2", bufs=3))
 
         one = keep.tile([P, 1], F32)
         nc.vector.memset(one[:], 1.0)
@@ -43,260 +52,278 @@ def tile_attention_prop_pa_t_kernel(
 
         planes = keep.tile([P, PASSES1 + 1, F], U8, align_bytes=64)
         nc.vector.memset(planes[:].bitcast(I32), 0)
+        ident_f32 = keep.tile([P, P], F32)
+        make_identity(nc, ident_f32[:])
+
         for q in range(4):
             nc.sync.dma_start(
                 out=planes[32 * q : 32 * q + 4, 0:PASSES1, :].bitcast(I32),
                 in_=w1_scales[:, 4 * q : 4 * q + 4, :].rearrange("g r n -> r g n").bitcast(I32),
             )
+
+        x_tiles = []
+
+        def load_x(group, pieces):
+            x_sb = x_pool.tile([P, 4, K1], BF16, name="x_sb")
+            rows = x[group * GROUP_ROWS : (group + 1) * GROUP_ROWS, :].rearrange("(p j) k -> p j k", j=4)
+            width = 4 // pieces
+            for i in range(pieces):
+                js = slice(i * width, (i + 1) * width)
+                nc.sync.dma_start(out=x_sb[:, js, :], in_=rows[:, js, :])
+            x_tiles.append(x_sb)
+
+        load_x(0, 2)
+        w1_raw = keep.tile([P, PASSES1, F], U32)
+        nc.sync.dma_start(
+            out=w1_raw[:].bitcast(I32),
+            in_=w1_words.rearrange("g p n t -> p g (n t)").bitcast(I32),
+        )
+        load_x(1, 1)
+        for q in range(4):
             nc.sync.dma_start(
                 out=planes[32 * q : 32 * q + 4, PASSES1, :].bitcast(I32),
                 in_=w2_scales[0, 4 * q : 4 * q + 4, :].bitcast(I32),
             )
+        w2_sb = keep.tile([P, F], U32, align_bytes=64)
+        nc.sync.dma_start(
+            out=w2_sb[:].bitcast(I32),
+            in_=w2_words[0].rearrange("p n t -> p (n t)").bitcast(I32),
+        )
+        for group in range(2, GROUPS):
+            load_x(group, 1)
 
-        with ExitStack() as main:
-            x_pool = main.enter_context(tc.tile_pool(name="x_pool", bufs=6))
-            x_tiles = []
-
-            def load_x(group):
-                x_sb = x_pool.tile([P, 4, K1], BF16, name="x_sb")
-                rows = x[group * GROUP_ROWS : (group + 1) * GROUP_ROWS, :]
-                nc.sync.dma_start(out=x_sb[:], in_=rows.rearrange("(p j) k -> p j k", j=4))
-                x_tiles.append(x_sb)
-
-            load_x(0)
-            w1_raw = keep.tile([P, PASSES1, F], U32)
-            nc.sync.dma_start(
-                out=w1_raw[:].bitcast(I32),
-                in_=w1_words.rearrange("g p n t -> p g (n t)").bitcast(I32),
+        b1_bf = keep.tile([P, PACK], BF16)
+        nc.gpsimd.dma_start(out=b1_bf[:], in_=b1.rearrange("(p t) -> p t", t=PACK))
+        vec_rows = keep.tile([P, P], BF16)
+        nc.vector.memset(vec_rows[:], 0.0)
+        for i, vec in enumerate((b2, gamma, beta)):
+            nc.gpsimd.dma_start(
+                out=vec_rows[F_BLOCKS * i : F_BLOCKS * (i + 1), :],
+                in_=vec.rearrange("(f c) -> f c", c=P),
             )
-            b1_bf = keep.tile([P, PACK], BF16)
-            nc.sync.dma_start(out=b1_bf[:], in_=b1.rearrange("(p t) -> p t", t=PACK))
-            vec_rows = keep.tile([P, P], BF16)
-            nc.vector.memset(vec_rows[:], 0.0)
-            for i, vec in enumerate((b2, gamma, beta)):
-                nc.sync.dma_start(
-                    out=vec_rows[F_BLOCKS * i : F_BLOCKS * (i + 1), :],
-                    in_=vec.rearrange("(f c) -> f c", c=P),
-                )
-            w2_sb = keep.tile([P, F], U32, align_bytes=64)
-            nc.sync.dma_start(
-                out=w2_sb[:].bitcast(I32),
-                in_=w2_words[0].rearrange("p n t -> p (n t)").bitcast(I32),
-            )
-            for group in range(1, GROUPS):
-                load_x(group)
+        ident_bf16 = keep.tile([P, P], BF16)
+        make_identity(nc, ident_bf16[:])
 
-            ident_f32 = keep.tile([P, P], F32)
-            make_identity(nc, ident_f32[:])
-            ident_bf16 = keep.tile([P, P], BF16)
-            make_identity(nc, ident_bf16[:])
+        planes1 = keep.tile([P, PASSES1, F], U8, align_bytes=64)
+        nc.vector.tensor_copy(
+            out=planes1[:].rearrange("p g (t m) -> p g m t", t=PACK),
+            in_=planes[:, 0:PASSES1, :].rearrange("p g (m t) -> p g m t", t=PACK),
+        )
+        w1_sb = keep.tile([P, PASSES1, F], U32, align_bytes=64)
+        nc.vector.tensor_copy(
+            out=w1_sb[:].bitcast(I32).rearrange("p g (t m) -> p g t m", t=PACK),
+            in_=w1_raw[:].bitcast(I32).rearrange("p g (m t) -> p g t m", t=PACK),
+        )
+        b1_cols = keep.tile([P, PACK], F32)
+        nc.vector.tensor_copy(out=b1_cols[:], in_=b1_bf[:])
 
-            planes1 = keep.tile([P, PASSES1, F], U8, align_bytes=64)
-            nc.vector.tensor_copy(
-                out=planes1[:].rearrange("p g (t m) -> p g m t", t=PACK),
-                in_=planes[:, 0:PASSES1, :].rearrange("p g (m t) -> p g m t", t=PACK),
-            )
-            w1_sb = keep.tile([P, PASSES1, F], U32, align_bytes=64)
-            nc.vector.tensor_copy(
-                out=w1_sb[:].bitcast(I32).rearrange("p g (t m) -> p g t m", t=PACK),
-                in_=w1_raw[:].bitcast(I32).rearrange("p g (m t) -> p g t m", t=PACK),
-            )
-            b1_cols = keep.tile([P, PACK], F32)
-            nc.vector.tensor_copy(out=b1_cols[:], in_=b1_bf[:])
+        h_codes = keep.tile([P, GROUPS, GROUP_ROWS], U32, align_bytes=64)
+        h_scales = keep.tile([P, GROUPS, GROUP_ROWS], U8, align_bytes=64)
+        h2t = keep.tile([P, F_BLOCKS, ROWS], F32)
+        sums = keep.tile([P, F_BLOCKS, GROUPS], F32)
+        squares = keep.tile([P, F_BLOCKS, GROUPS], F32)
+        vec_cols = keep.tile([P, 3 * F_BLOCKS], F32)
+        b2_slope = keep.tile([P, F_BLOCKS], F32)
+        mean = keep.tile([P, F_BLOCKS], F32)
+        var = keep.tile([P, F_BLOCKS], F32)
+        mean_sq = keep.tile([P, F_BLOCKS], F32)
+        std = keep.tile([P, F_BLOCKS], F32)
+        gain = keep.tile([P, F_BLOCKS], F32)
+        shift = keep.tile([P, F_BLOCKS], F32)
 
-            h2t = keep.tile([P, F_BLOCKS, ROWS], F32)
-            sums = keep.tile([P, F_BLOCKS, GROUPS], F32)
-            squares = keep.tile([P, F_BLOCKS, GROUPS], F32)
-            vec_cols = keep.tile([P, 3 * F_BLOCKS], F32)
-            b2_slope = keep.tile([P, F_BLOCKS], F32)
+        x_grouped = {}
+        x_codes = {}
+        v_tiles = {}
+        h_grouped = {}
 
-            with tc.psum_pool(name="ps_setup", bufs=1) as ps_setup:
-                vec_ps = ps_setup.tile([P, P], BF16, name="vec_ps")
-                nc.tensor.transpose(vec_ps[:], vec_rows[:], ident_bf16[:])
-                nc.vector.tensor_copy(out=vec_cols[:], in_=vec_ps[:, 0 : 3 * F_BLOCKS])
+        def vectors_to_columns():
+            vec_ps = ps_acc2.tile([P, P], BF16, name="acc2")
+            nc.tensor.transpose(vec_ps[:], vec_rows[:], ident_bf16[:])
+            nc.vector.tensor_copy(out=vec_cols[:], in_=vec_ps[:, 0 : 3 * F_BLOCKS])
             nc.vector.tensor_scalar_mul(out=b2_slope[:], in0=vec_cols[:, 0:F_BLOCKS], scalar1=SLOPE)
 
-            xq = main.enter_context(tc.tile_pool(name="xq", bufs=4))
-            hq = main.enter_context(tc.tile_pool(name="hq", bufs=3))
-            v_pool = main.enter_context(tc.tile_pool(name="v_pool", bufs=3))
-            work = main.enter_context(tc.tile_pool(name="work", bufs=4))
-            ps_xt = main.enter_context(tc.psum_pool(name="ps_xt", bufs=2))
-            ps_acc1 = main.enter_context(tc.psum_pool(name="ps_acc1", bufs=3))
-            ps_acc2 = main.enter_context(tc.psum_pool(name="ps_acc2", bufs=3))
+        def transpose_x(group):
+            x_words = x_tiles[group][:].bitcast(F32)
+            for g in range(PASSES1):
+                grouped = xg_pool.tile([P, GROUP_ROWS, PACK], BF16, name="x_grouped", align_bytes=64)
+                for half in range(2):
+                    xt = ps_xt.tile([P, 2, HALF_ROWS], F32, name="xt")
+                    for jj in range(2):
+                        j = 2 * half + jj
+                        for u in range(2):
+                            nc.tensor.transpose(
+                                xt[:, u, jj * P : (jj + 1) * P],
+                                x_words[:, j, 256 * g + u : 256 * (g + 1) : 2],
+                                ident_f32[:],
+                            )
+                    dst = grouped[:, half * HALF_ROWS : (half + 1) * HALF_ROWS, :].bitcast(F32)
+                    src = xt[:].rearrange("p u r -> p r u")
+                    if half == 0 or g == 0:
+                        nc.scalar.copy(out=dst, in_=src)
+                    else:
+                        nc.vector.tensor_copy(out=dst, in_=src)
+                x_grouped[(group, g)] = grouped
 
-            x_grouped = {}
-            x_codes = {}
-            v_tiles = {}
-            h_grouped = {}
-
-            def transpose_x(group):
-                x_words = x_tiles[group][:].bitcast(F32)
-                for g in range(PASSES1):
-                    grouped = xq.tile([P, GROUP_ROWS, PACK], BF16, name="x_grouped", align_bytes=64)
-                    for half in range(2):
-                        xt = ps_xt.tile([P, 2, HALF_ROWS], F32, name="xt")
-                        for jj in range(2):
-                            j = 2 * half + jj
-                            for u in range(2):
-                                nc.tensor.transpose(
-                                    xt[:, u, jj * P : (jj + 1) * P],
-                                    x_words[:, j, 256 * g + u : 256 * (g + 1) : 2],
-                                    ident_f32[:],
-                                )
-                        dst = grouped[:, half * HALF_ROWS : (half + 1) * HALF_ROWS, :].bitcast(F32)
-                        src = xt[:].rearrange("p u r -> p r u")
-                        if half == 0:
-                            nc.scalar.copy(out=dst, in_=src)
-                        else:
-                            nc.vector.tensor_copy(out=dst, in_=src)
-                    x_grouped[(group, g)] = grouped
-
-            def quantise_x(group):
-                for g in range(PASSES1):
-                    grouped = x_grouped.pop((group, g))
-                    codes = xq.tile([P, GROUP_ROWS], U32, name="x_code", align_bytes=64)
-                    scales = xq.tile([P, GROUP_ROWS], U8, name="x_scale", align_bytes=64)
-                    nc.vector.quantize_mx(
-                        out=codes[:].bitcast(FP8X4),
-                        scales=scales[:],
-                        in_=grouped[:].rearrange("p r t -> p (r t)"),
-                    )
-                    x_codes[(group, g)] = (codes, scales)
-
-            def layer1(group):
-                v = v_pool.tile([P, PACK, GROUP_ROWS], F32, name="v")
-                for t in range(PACK):
-                    feats = slice(t * P, (t + 1) * P)
-                    acc1 = ps_acc1.tile([P, GROUP_ROWS], F32, name="acc1")
-                    for g in range(PASSES1):
-                        codes, scales = x_codes[(group, g)]
-                        nc.tensor.matmul_mx(
-                            out=acc1[:],
-                            lhsT=w1_sb[:, g, feats].bitcast(FP8X4),
-                            lhsT_scale=planes1[:, g, feats],
-                            rhs=codes[:].bitcast(FP8X4),
-                            rhs_scale=scales[:],
-                            start=(g == 0),
-                            stop=(g == PASSES1 - 1),
-                        )
-                    nc.scalar.activation(
-                        out=v[:, t, :], in_=acc1[:], func=ACT.Identity, bias=b1_cols[:, t : t + 1]
-                    )
-                for g in range(PASSES1):
-                    x_codes.pop((group, g))
-                v_tiles[group] = v
-
-            def leaky1(group):
-                v_rt = v_tiles.pop(group)[:].rearrange("p t r -> p r t")
-                grouped = hq.tile([P, GROUP_ROWS, PACK], BF16, name="h_grouped", align_bytes=64)
-                nc.vector.scalar_tensor_tensor(
-                    out=grouped[:], in0=v_rt, scalar=SLOPE, in1=v_rt, op0=ALU.mult, op1=ALU.max
-                )
-                h_grouped[group] = grouped
-
-            def layer2(group):
-                grouped = h_grouped.pop(group)
-                codes = hq.tile([P, GROUP_ROWS], U32, name="h_code", align_bytes=64)
-                scales = hq.tile([P, GROUP_ROWS], U8, name="h_scale", align_bytes=64)
+        def quantise_x(group):
+            for g in range(PASSES1):
+                grouped = x_grouped.pop((group, g))
+                codes = xc_pool.tile([P, GROUP_ROWS], U32, name="x_code", align_bytes=64)
+                scales = xc_pool.tile([P, GROUP_ROWS], U8, name="x_scale", align_bytes=64)
                 nc.vector.quantize_mx(
                     out=codes[:].bitcast(FP8X4),
                     scales=scales[:],
                     in_=grouped[:].rearrange("p r t -> p (r t)"),
                 )
-                cols = slice(group * GROUP_ROWS, (group + 1) * GROUP_ROWS)
-                for fb in range(F_BLOCKS):
-                    feats = slice(fb * P, (fb + 1) * P)
-                    acc2 = ps_acc2.tile([P, GROUP_ROWS], F32, name="acc2")
+                x_codes[(group, g)] = (codes, scales)
+
+        def layer1(group):
+            v = v_pool.tile([P, PACK, GROUP_ROWS], F32, name="v")
+            for t in range(PACK):
+                feats = slice(t * P, (t + 1) * P)
+                acc1 = ps_acc1.tile([P, GROUP_ROWS], F32, name="acc1")
+                for g in range(PASSES1):
+                    codes, scales = x_codes[(group, g)]
                     nc.tensor.matmul_mx(
-                        out=acc2[:],
-                        lhsT=w2_sb[:, feats].bitcast(FP8X4),
-                        lhsT_scale=planes[:, PASSES1, feats],
+                        out=acc1[:],
+                        lhsT=w1_sb[:, g, feats].bitcast(FP8X4),
+                        lhsT_scale=planes1[:, g, feats],
                         rhs=codes[:].bitcast(FP8X4),
                         rhs_scale=scales[:],
-                        start=True,
-                        stop=True,
+                        start=(g == 0),
+                        stop=(g == PASSES1 - 1),
                     )
-                    low = work.tile([P, GROUP_ROWS], F32, name="low")
-                    nc.scalar.activation(
-                        out=low[:],
-                        in_=acc2[:],
-                        func=ACT.Identity,
-                        scale=SLOPE,
-                        bias=b2_slope[:, fb : fb + 1],
-                    )
-                    nc.vector.scalar_tensor_tensor(
-                        out=h2t[:, fb, cols],
-                        in0=acc2[:],
-                        scalar=vec_cols[:, fb : fb + 1],
-                        in1=low[:],
-                        op0=ALU.add,
-                        op1=ALU.max,
-                        accum_out=sums[:, fb, group : group + 1],
-                    )
-                    unread = work.tile([P, GROUP_ROWS], BF16, name="unread")
-                    nc.scalar.activation(
-                        out=unread[:],
-                        in_=h2t[:, fb, cols],
-                        func=ACT.Square,
-                        accum_out=squares[:, fb, group : group + 1],
-                    )
+                nc.scalar.activation(
+                    out=v[:, t, :], in_=acc1[:], func=ACT.Identity, bias=b1_cols[:, t : t + 1]
+                )
+            v_tiles[group] = v
 
-            for step in range(GROUPS + 3):
-                if step < GROUPS:
-                    transpose_x(step)
-                if 0 <= step - 1 < GROUPS:
-                    quantise_x(step - 1)
-                    layer1(step - 1)
-                if 0 <= step - 2 < GROUPS:
-                    leaky1(step - 2)
-                if 0 <= step - 3 < GROUPS:
-                    layer2(step - 3)
+        def leaky1(group):
+            v_rt = v_tiles.pop(group)[:].rearrange("p t r -> p r t")
+            grouped = hg_pool.tile([P, GROUP_ROWS, PACK], BF16, name="h_grouped", align_bytes=64)
+            nc.vector.scalar_tensor_tensor(
+                out=grouped[:], in0=v_rt, scalar=SLOPE, in1=v_rt, op0=ALU.mult, op1=ALU.max
+            )
+            h_grouped[group] = grouped
 
-        mean = keep.tile([P, F_BLOCKS], F32)
-        nc.vector.tensor_reduce(out=mean[:], in_=sums[:], axis=mybir.AxisListType.X, op=ALU.add)
-        nc.vector.tensor_scalar_mul(out=mean[:], in0=mean[:], scalar1=1.0 / ROWS)
-        var = keep.tile([P, F_BLOCKS], F32)
-        nc.vector.tensor_reduce(out=var[:], in_=squares[:], axis=mybir.AxisListType.X, op=ALU.add)
-        mean_sq = keep.tile([P, F_BLOCKS], F32)
-        nc.vector.tensor_mul(out=mean_sq[:], in0=mean[:], in1=mean[:])
-        nc.vector.scalar_tensor_tensor(
-            out=var[:], in0=var[:], scalar=1.0 / ROWS, in1=mean_sq[:], op0=ALU.mult, op1=ALU.subtract
-        )
-        nc.vector.tensor_scalar_add(out=var[:], in0=var[:], scalar1=EPS)
-        std = keep.tile([P, F_BLOCKS], F32)
-        nc.scalar.activation(out=std[:], in_=var[:], func=ACT.Sqrt)
-        gain = keep.tile([P, F_BLOCKS], F32)
-        nc.vector.reciprocal(out=gain[:], in_=std[:])
-        nc.vector.tensor_mul(out=gain[:], in0=gain[:], in1=vec_cols[:, F_BLOCKS : 2 * F_BLOCKS])
-        shift = keep.tile([P, F_BLOCKS], F32)
-        nc.vector.tensor_mul(out=shift[:], in0=mean[:], in1=gain[:])
-        nc.vector.tensor_sub(out=shift[:], in0=vec_cols[:, 2 * F_BLOCKS : 3 * F_BLOCKS], in1=shift[:])
+        def quantise_h(group):
+            nc.vector.quantize_mx(
+                out=h_codes[:, group, :].bitcast(FP8X4),
+                scales=h_scales[:, group, :],
+                in_=h_grouped.pop(group)[:].rearrange("p r t -> p (r t)"),
+            )
 
-        with ExitStack() as tail:
-            ps_out = tail.enter_context(tc.psum_pool(name="ps_out", bufs=4))
-            stage_pool = tail.enter_context(tc.tile_pool(name="stage_pool", bufs=3))
-            for group in range(GROUPS):
-                cols = slice(group * GROUP_ROWS, (group + 1) * GROUP_ROWS)
-                for fb in range(F_BLOCKS):
-                    nc.vector.tensor_scalar(
-                        out=h2t[:, fb, cols],
-                        in0=h2t[:, fb, cols],
-                        scalar1=gain[:, fb : fb + 1],
-                        scalar2=shift[:, fb : fb + 1],
-                        op0=ALU.mult,
-                        op1=ALU.add,
-                    )
-                stage = stage_pool.tile([P, 4, F], F32, name="stage")
-                for j in range(4):
-                    first = group * GROUP_ROWS + j * P
-                    ot = ps_out.tile([P, F], F32, name="ot")
-                    for fb in range(F_BLOCKS):
+        def layer2(fb, group):
+            cols = slice(group * GROUP_ROWS, (group + 1) * GROUP_ROWS)
+            feats = slice(fb * P, (fb + 1) * P)
+            acc2 = ps_acc2.tile([P, GROUP_ROWS], F32, name="acc2")
+            nc.tensor.matmul_mx(
+                out=acc2[:],
+                lhsT=w2_sb[:, feats].bitcast(FP8X4),
+                lhsT_scale=planes[:, PASSES1, feats],
+                rhs=h_codes[:, group, :].bitcast(FP8X4),
+                rhs_scale=h_scales[:, group, :],
+                start=True,
+                stop=True,
+            )
+            low = work.tile([P, GROUP_ROWS], F32, name="low")
+            nc.scalar.activation(
+                out=low[:], in_=acc2[:], func=ACT.Identity, scale=SLOPE, bias=b2_slope[:, fb : fb + 1]
+            )
+            nc.vector.scalar_tensor_tensor(
+                out=h2t[:, fb, cols],
+                in0=acc2[:],
+                scalar=vec_cols[:, fb : fb + 1],
+                in1=low[:],
+                op0=ALU.add,
+                op1=ALU.max,
+                accum_out=sums[:, fb, group : group + 1],
+            )
+            unread = work.tile([P, GROUP_ROWS], BF16, name="unread")
+            nc.scalar.activation(
+                out=unread[:],
+                in_=h2t[:, fb, cols],
+                func=ACT.Square,
+                accum_out=squares[:, fb, group : group + 1],
+            )
+
+        def statistics(lo, hi):
+            s = slice(lo, hi)
+            nc.vector.tensor_reduce(out=mean[:, s], in_=sums[:, s, :], axis=mybir.AxisListType.X, op=ALU.add)
+            nc.vector.tensor_scalar_mul(out=mean[:, s], in0=mean[:, s], scalar1=1.0 / ROWS)
+            nc.vector.tensor_reduce(out=var[:, s], in_=squares[:, s, :], axis=mybir.AxisListType.X, op=ALU.add)
+            nc.vector.tensor_mul(out=mean_sq[:, s], in0=mean[:, s], in1=mean[:, s])
+            nc.vector.scalar_tensor_tensor(
+                out=var[:, s], in0=var[:, s], scalar=1.0 / ROWS, in1=mean_sq[:, s],
+                op0=ALU.mult, op1=ALU.subtract,
+            )
+            nc.vector.tensor_scalar_add(out=var[:, s], in0=var[:, s], scalar1=EPS)
+            nc.scalar.activation(out=std[:, s], in_=var[:, s], func=ACT.Sqrt)
+            nc.vector.reciprocal(out=gain[:, s], in_=std[:, s])
+            nc.vector.tensor_mul(out=gain[:, s], in0=gain[:, s], in1=vec_cols[:, F_BLOCKS + lo : F_BLOCKS + hi])
+            nc.vector.tensor_mul(out=shift[:, s], in0=mean[:, s], in1=gain[:, s])
+            nc.vector.tensor_sub(
+                out=shift[:, s], in0=vec_cols[:, 2 * F_BLOCKS + lo : 2 * F_BLOCKS + hi], in1=shift[:, s]
+            )
+
+        counts = {"bank": 0, "copy": 0}
+
+        def output(lo, hi, group, on_gpsimd, scalar_every):
+            cols = slice(group * GROUP_ROWS, (group + 1) * GROUP_ROWS)
+            blocks = hi - lo
+            for fb in range(lo, hi):
+                engine = nc.gpsimd if on_gpsimd else nc.vector
+                engine.tensor_scalar(
+                    out=h2t[:, fb, cols],
+                    in0=h2t[:, fb, cols],
+                    scalar1=gain[:, fb : fb + 1],
+                    scalar2=shift[:, fb : fb + 1],
+                    op0=ALU.mult,
+                    op1=ALU.add,
+                )
+            stage = x_pool.tile([P, 4, blocks * P], F32, name="x_sb")
+            per_bank = 4 // blocks
+            for first_j in range(0, 4, per_bank):
+                if counts["bank"] % 5 < 2:
+                    ot = ps_xt.tile([P, per_bank, blocks * P], F32, name="xt")
+                else:
+                    ot = ps_acc1.tile([P, per_bank, blocks * P], F32, name="acc1")
+                counts["bank"] += 1
+                for jj in range(per_bank):
+                    first = group * GROUP_ROWS + (first_j + jj) * P
+                    for fb in range(lo, hi):
                         nc.tensor.transpose(
-                            ot[:, fb * P : (fb + 1) * P], h2t[:, fb, first : first + P], ident_f32[:]
+                            ot[:, jj, (fb - lo) * P : (fb - lo + 1) * P],
+                            h2t[:, fb, first : first + P],
+                            ident_f32[:],
                         )
-                    if j == 3:
-                        nc.vector.tensor_copy(out=stage[:, j, :], in_=ot[:])
-                    else:
-                        nc.scalar.copy(out=stage[:, j, :], in_=ot[:])
-                rows = out[group * GROUP_ROWS : (group + 1) * GROUP_ROWS, :]
-                nc.sync.dma_start(out=rows.rearrange("(p j) f -> p j f", j=4), in_=stage[:])
+                if counts["copy"] % scalar_every == 0:
+                    nc.scalar.copy(out=stage[:, first_j : first_j + per_bank, :], in_=ot[:])
+                else:
+                    nc.vector.tensor_copy(out=stage[:, first_j : first_j + per_bank, :], in_=ot[:])
+                counts["copy"] += 1
+            rows = out[group * GROUP_ROWS : (group + 1) * GROUP_ROWS, lo * P : hi * P]
+            nc.sync.dma_start(out=rows.rearrange("(p j) f -> p j f", j=4), in_=stage[:])
+
+        for step in range(GROUPS + 3):
+            if step < GROUPS:
+                transpose_x(step)
+            if 0 <= step - 1 < GROUPS:
+                quantise_x(step - 1)
+                layer1(step - 1)
+            if 0 <= step - 2 < GROUPS:
+                leaky1(step - 2)
+            if step == 3:
+                vectors_to_columns()
+            if 0 <= step - 3 < GROUPS:
+                quantise_h(step - 3)
+                layer2(0, step - 3)
+                layer2(1, step - 3)
+
+        statistics(0, 2)
+        for group in range(GROUPS):
+            layer2(2, group)
+            layer2(3, group)
+            output(0, 2, group, True, 4)
+        statistics(2, 4)
+        for group in range(GROUPS):
+            output(2, 4, group, False, 1)

@@ -63,22 +63,26 @@ def tile_attention_prop_pa_t_kernel(
 
         x_tiles = []
 
-        def load_x(group, pieces):
+        def load_x(group, in_pieces):
             x_sb = x_pool.tile([P, 4, K1], BF16, name="x_sb")
             rows = x[group * GROUP_ROWS : (group + 1) * GROUP_ROWS, :].rearrange("(p j) k -> p j k", j=4)
-            width = 4 // pieces
-            for i in range(pieces):
-                js = slice(i * width, (i + 1) * width)
-                nc.sync.dma_start(out=x_sb[:, js, :], in_=rows[:, js, :])
+            if in_pieces:
+                for g in range(PASSES1):
+                    ks = slice(g * K_PASS, (g + 1) * K_PASS)
+                    for half in range(2):
+                        js = slice(2 * half, 2 * half + 2)
+                        nc.sync.dma_start(out=x_sb[:, js, ks], in_=rows[:, js, ks])
+            else:
+                nc.sync.dma_start(out=x_sb[:], in_=rows)
             x_tiles.append(x_sb)
 
-        load_x(0, 2)
+        load_x(0, True)
         w1_raw = keep.tile([P, PASSES1, F], U32)
         nc.sync.dma_start(
             out=w1_raw[:].bitcast(I32),
             in_=w1_words.rearrange("g p n t -> p g (n t)").bitcast(I32),
         )
-        load_x(1, 1)
+        load_x(1, False)
         for q in range(4):
             nc.sync.dma_start(
                 out=planes[32 * q : 32 * q + 4, PASSES1, :].bitcast(I32),
@@ -90,7 +94,7 @@ def tile_attention_prop_pa_t_kernel(
             in_=w2_words[0].rearrange("p n t -> p (n t)").bitcast(I32),
         )
         for group in range(2, GROUPS):
-            load_x(group, 1)
+            load_x(group, False)
 
         b1_bf = keep.tile([P, PACK], BF16)
         nc.gpsimd.dma_start(out=b1_bf[:], in_=b1.rearrange("(p t) -> p t", t=PACK))
@@ -120,11 +124,12 @@ def tile_attention_prop_pa_t_kernel(
         h_codes = keep.tile([P, GROUPS, GROUP_ROWS], U32, align_bytes=64)
         h_scales = keep.tile([P, GROUPS, GROUP_ROWS], U8, align_bytes=64)
         h2t = keep.tile([P, F_BLOCKS, ROWS], F32)
-        sums = keep.tile([P, F_BLOCKS, GROUPS], F32)
-        squares = keep.tile([P, F_BLOCKS, GROUPS], F32)
+        moments = keep.tile([P, 2, F_BLOCKS, GROUPS], F32)
+        totals = keep.tile([P, 2, F_BLOCKS], F32)
+        eps_col = keep.tile([P, 1], F32)
+        nc.vector.tensor_scalar(out=eps_col[:], in0=one[:], scalar1=0.0, scalar2=EPS, op0=ALU.mult, op1=ALU.add)
         vec_cols = keep.tile([P, 3 * F_BLOCKS], F32)
         b2_slope = keep.tile([P, F_BLOCKS], F32)
-        mean = keep.tile([P, F_BLOCKS], F32)
         var = keep.tile([P, F_BLOCKS], F32)
         mean_sq = keep.tile([P, F_BLOCKS], F32)
         std = keep.tile([P, F_BLOCKS], F32)
@@ -236,33 +241,35 @@ def tile_attention_prop_pa_t_kernel(
                 in1=low[:],
                 op0=ALU.add,
                 op1=ALU.max,
-                accum_out=sums[:, fb, group : group + 1],
+                accum_out=moments[:, 0, fb, group : group + 1],
             )
             unread = work.tile([P, GROUP_ROWS], BF16, name="unread")
             nc.scalar.activation(
                 out=unread[:],
                 in_=h2t[:, fb, cols],
                 func=ACT.Square,
-                accum_out=squares[:, fb, group : group + 1],
+                accum_out=moments[:, 1, fb, group : group + 1],
             )
 
         def statistics(lo, hi):
             s = slice(lo, hi)
-            nc.vector.tensor_reduce(out=mean[:, s], in_=sums[:, s, :], axis=mybir.AxisListType.X, op=ALU.add)
-            nc.vector.tensor_scalar_mul(out=mean[:, s], in0=mean[:, s], scalar1=1.0 / ROWS)
-            nc.vector.tensor_reduce(out=var[:, s], in_=squares[:, s, :], axis=mybir.AxisListType.X, op=ALU.add)
-            nc.vector.tensor_mul(out=mean_sq[:, s], in0=mean[:, s], in1=mean[:, s])
+            nc.vector.tensor_reduce(
+                out=totals[:, :, s], in_=moments[:, :, s, :], axis=mybir.AxisListType.X, op=ALU.add
+            )
+            nc.vector.tensor_mul(out=mean_sq[:, s], in0=totals[:, 0, s], in1=totals[:, 0, s])
             nc.vector.scalar_tensor_tensor(
-                out=var[:, s], in0=var[:, s], scalar=1.0 / ROWS, in1=mean_sq[:, s],
+                out=var[:, s], in0=totals[:, 1, s], scalar=float(ROWS), in1=mean_sq[:, s],
                 op0=ALU.mult, op1=ALU.subtract,
             )
-            nc.vector.tensor_scalar_add(out=var[:, s], in0=var[:, s], scalar1=EPS)
-            nc.scalar.activation(out=std[:, s], in_=var[:, s], func=ACT.Sqrt)
+            nc.scalar.activation(
+                out=std[:, s], in_=var[:, s], func=ACT.Sqrt, scale=1.0 / (ROWS * ROWS), bias=eps_col[:]
+            )
             nc.vector.reciprocal(out=gain[:, s], in_=std[:, s])
             nc.vector.tensor_mul(out=gain[:, s], in0=gain[:, s], in1=vec_cols[:, F_BLOCKS + lo : F_BLOCKS + hi])
-            nc.vector.tensor_mul(out=shift[:, s], in0=mean[:, s], in1=gain[:, s])
-            nc.vector.tensor_sub(
-                out=shift[:, s], in0=vec_cols[:, 2 * F_BLOCKS + lo : 2 * F_BLOCKS + hi], in1=shift[:, s]
+            nc.vector.tensor_mul(out=shift[:, s], in0=totals[:, 0, s], in1=gain[:, s])
+            nc.vector.scalar_tensor_tensor(
+                out=shift[:, s], in0=shift[:, s], scalar=-1.0 / ROWS,
+                in1=vec_cols[:, 2 * F_BLOCKS + lo : 2 * F_BLOCKS + hi], op0=ALU.mult, op1=ALU.add,
             )
 
         counts = {"bank": 0, "copy": 0}
@@ -281,6 +288,9 @@ def tile_attention_prop_pa_t_kernel(
                     op1=ALU.add,
                 )
             stage = x_pool.tile([P, 4, blocks * P], F32, name="x_sb")
+            rows = out[group * GROUP_ROWS : (group + 1) * GROUP_ROWS, lo * P : hi * P].rearrange(
+                "(p j) f -> p j f", j=4
+            )
             per_bank = 4 // blocks
             for first_j in range(0, 4, per_bank):
                 if counts["bank"] % 5 < 2:
@@ -301,8 +311,11 @@ def tile_attention_prop_pa_t_kernel(
                 else:
                     nc.vector.tensor_copy(out=stage[:, first_j : first_j + per_bank, :], in_=ot[:])
                 counts["copy"] += 1
-            rows = out[group * GROUP_ROWS : (group + 1) * GROUP_ROWS, lo * P : hi * P]
-            nc.sync.dma_start(out=rows.rearrange("(p j) f -> p j f", j=4), in_=stage[:])
+                if not on_gpsimd:
+                    js = slice(first_j, first_j + per_bank)
+                    nc.sync.dma_start(out=rows[:, js, :], in_=stage[:, js, :])
+            if on_gpsimd:
+                nc.sync.dma_start(out=rows, in_=stage[:])
 
         for step in range(GROUPS + 3):
             if step < GROUPS:

@@ -274,7 +274,7 @@ def tile_attention_prop_pa_t_kernel(
 
         counts = {"bank": 0, "copy": 0}
 
-        def output(lo, hi, group, on_gpsimd, scalar_every):
+        def output(lo, hi, group, on_gpsimd, scalar_of_four):
             cols = slice(group * GROUP_ROWS, (group + 1) * GROUP_ROWS)
             blocks = hi - lo
             for fb in range(lo, hi):
@@ -306,7 +306,7 @@ def tile_attention_prop_pa_t_kernel(
                             h2t[:, fb, first : first + P],
                             ident_f32[:],
                         )
-                if counts["copy"] % scalar_every == 0:
+                if counts["copy"] % 4 < scalar_of_four:
                     nc.scalar.copy(out=stage[:, first_j : first_j + per_bank, :], in_=ot[:])
                 else:
                     nc.vector.tensor_copy(out=stage[:, first_j : first_j + per_bank, :], in_=ot[:])
@@ -336,7 +336,7 @@ def tile_attention_prop_pa_t_kernel(
         for group in range(GROUPS):
             layer2(2, group)
             layer2(3, group)
-            output(0, 2, group, True, 4)
+            output(0, 2, group, True, 0)
         statistics(2, 4)
         for group in range(GROUPS):
-            output(2, 4, group, False, 1)
+            output(2, 4, group, False, 3)

@@ -26,6 +26,14 @@ F_BLOCKS = F // P
 SLOPE = 0.01
 EPS = 1e-5
 
+PHASES = ((0, 1, 2), (3,))
+X_COPIES_ON_SCALAR = (3, 2)
+LOADS = (0, "w1", 1, "w2", 2, 3, 4, 5, 6, 7)
+PIECES = 1
+LAG = 2
+NORM_GPSIMD_OF = 2
+COPY_SCALAR_OF = 2
+
 FLOPS = 2 * ROWS * K1 * F + 2 * ROWS * F * F
 
 
@@ -76,25 +84,33 @@ def tile_attention_prop_pa_t_kernel(
                 nc.sync.dma_start(out=x_sb[:], in_=rows)
             x_tiles.append(x_sb)
 
-        load_x(0, True)
         w1_raw = keep.tile([P, PASSES1, F], U32)
-        nc.sync.dma_start(
-            out=w1_raw[:].bitcast(I32),
-            in_=w1_words.rearrange("g p n t -> p g (n t)").bitcast(I32),
-        )
-        load_x(1, False)
-        for q in range(4):
-            nc.sync.dma_start(
-                out=planes[32 * q : 32 * q + 4, PASSES1, :].bitcast(I32),
-                in_=w2_scales[0, 4 * q : 4 * q + 4, :].bitcast(I32),
-            )
         w2_sb = keep.tile([P, F], U32, align_bytes=64)
-        nc.sync.dma_start(
-            out=w2_sb[:].bitcast(I32),
-            in_=w2_words[0].rearrange("p n t -> p (n t)").bitcast(I32),
-        )
-        for group in range(2, GROUPS):
-            load_x(group, False)
+
+        def load_w1():
+            nc.sync.dma_start(
+                out=w1_raw[:].bitcast(I32),
+                in_=w1_words.rearrange("g p n t -> p g (n t)").bitcast(I32),
+            )
+
+        def load_w2():
+            for q in range(4):
+                nc.sync.dma_start(
+                    out=planes[32 * q : 32 * q + 4, PASSES1, :].bitcast(I32),
+                    in_=w2_scales[0, 4 * q : 4 * q + 4, :].bitcast(I32),
+                )
+            nc.sync.dma_start(
+                out=w2_sb[:].bitcast(I32),
+                in_=w2_words[0].rearrange("p n t -> p (n t)").bitcast(I32),
+            )
+
+        for what in LOADS:
+            if what == "w1":
+                load_w1()
+            elif what == "w2":
+                load_w2()
+            else:
+                load_x(what, what < PIECES)
 
         b1_bf = keep.tile([P, PACK], BF16)
         nc.gpsimd.dma_start(out=b1_bf[:], in_=b1.rearrange("(p t) -> p t", t=PACK))
@@ -163,7 +179,7 @@ def tile_attention_prop_pa_t_kernel(
                             )
                     dst = grouped[:, half * HALF_ROWS : (half + 1) * HALF_ROWS, :].bitcast(F32)
                     src = xt[:].rearrange("p u r -> p r u")
-                    if half == 0 or g == 0:
+                    if 2 * g + half < X_COPIES_ON_SCALAR[group % 2]:
                         nc.scalar.copy(out=dst, in_=src)
                     else:
                         nc.vector.tensor_copy(out=dst, in_=src)
@@ -272,12 +288,18 @@ def tile_attention_prop_pa_t_kernel(
                 in1=vec_cols[:, 2 * F_BLOCKS + lo : 2 * F_BLOCKS + hi], op0=ALU.mult, op1=ALU.add,
             )
 
-        counts = {"bank": 0, "copy": 0}
+        counts = {"bank": 0, "copy": 0, "norm": 0}
 
-        def output(lo, hi, group, on_gpsimd, scalar_of_four):
+        def output(blocks, group, last):
             cols = slice(group * GROUP_ROWS, (group + 1) * GROUP_ROWS)
-            blocks = hi - lo
-            for fb in range(lo, hi):
+            lo = blocks[0]
+            stage = x_pool.tile([P, 4, len(blocks) * P], F32, name="x_sb")
+            rows = out[group * GROUP_ROWS : (group + 1) * GROUP_ROWS, lo * P : (lo + len(blocks)) * P].rearrange(
+                "(p j) f -> p j f", j=4
+            )
+            for fb in blocks:
+                on_gpsimd = (not last) and counts["norm"] % NORM_GPSIMD_OF == 0
+                counts["norm"] += 1
                 engine = nc.gpsimd if on_gpsimd else nc.vector
                 engine.tensor_scalar(
                     out=h2t[:, fb, cols],
@@ -287,35 +309,22 @@ def tile_attention_prop_pa_t_kernel(
                     op0=ALU.mult,
                     op1=ALU.add,
                 )
-            stage = x_pool.tile([P, 4, blocks * P], F32, name="x_sb")
-            rows = out[group * GROUP_ROWS : (group + 1) * GROUP_ROWS, lo * P : hi * P].rearrange(
-                "(p j) f -> p j f", j=4
-            )
-            per_bank = 4 // blocks
-            for first_j in range(0, 4, per_bank):
+            for fb in blocks:
                 if counts["bank"] % 5 < 2:
-                    ot = ps_xt.tile([P, per_bank, blocks * P], F32, name="xt")
+                    ot = ps_xt.tile([P, 4, P], F32, name="xt")
                 else:
-                    ot = ps_acc1.tile([P, per_bank, blocks * P], F32, name="acc1")
+                    ot = ps_acc1.tile([P, 4, P], F32, name="acc1")
                 counts["bank"] += 1
-                for jj in range(per_bank):
-                    first = group * GROUP_ROWS + (first_j + jj) * P
-                    for fb in range(lo, hi):
-                        nc.tensor.transpose(
-                            ot[:, jj, (fb - lo) * P : (fb - lo + 1) * P],
-                            h2t[:, fb, first : first + P],
-                            ident_f32[:],
-                        )
-                if counts["copy"] % 4 < scalar_of_four:
-                    nc.scalar.copy(out=stage[:, first_j : first_j + per_bank, :], in_=ot[:])
+                for j in range(4):
+                    first = group * GROUP_ROWS + j * P
+                    nc.tensor.transpose(ot[:, j, :], h2t[:, fb, first : first + P], ident_f32[:])
+                dst = stage[:, :, (fb - lo) * P : (fb - lo + 1) * P]
+                if counts["copy"] % COPY_SCALAR_OF == 0:
+                    nc.scalar.copy(out=dst, in_=ot[:])
                 else:
-                    nc.vector.tensor_copy(out=stage[:, first_j : first_j + per_bank, :], in_=ot[:])
+                    nc.vector.tensor_copy(out=dst, in_=ot[:])
                 counts["copy"] += 1
-                if not on_gpsimd:
-                    js = slice(first_j, first_j + per_bank)
-                    nc.sync.dma_start(out=rows[:, js, :], in_=stage[:, js, :])
-            if on_gpsimd:
-                nc.sync.dma_start(out=rows, in_=stage[:])
+            nc.sync.dma_start(out=rows, in_=stage[:])
 
         for step in range(GROUPS + 3):
             if step < GROUPS:
@@ -329,14 +338,18 @@ def tile_attention_prop_pa_t_kernel(
                 vectors_to_columns()
             if 0 <= step - 3 < GROUPS:
                 quantise_h(step - 3)
-                layer2(0, step - 3)
-                layer2(1, step - 3)
+                for fb in PHASES[0]:
+                    layer2(fb, step - 3)
 
-        statistics(0, 2)
+        statistics(PHASES[0][0], PHASES[0][-1] + 1)
+        for i in range(1, len(PHASES)):
+            for group in range(GROUPS):
+                for fb in PHASES[i]:
+                    layer2(fb, group)
+                if group >= LAG:
+                    output(PHASES[i - 1], group - LAG, False)
+            statistics(PHASES[i][0], PHASES[i][-1] + 1)
+            for group in range(GROUPS - LAG, GROUPS):
+                output(PHASES[i - 1], group, False)
         for group in range(GROUPS):
-            layer2(2, group)
-            layer2(3, group)
-            output(0, 2, group, True, 0)
-        statistics(2, 4)
-        for group in range(GROUPS):
-            output(2, 4, group, False, 3)
+            output(PHASES[-1], group, True)

@@ -24,6 +24,7 @@ HALF_ROWS = 2 * P
 GROUPS = ROWS // GROUP_ROWS
 F_BLOCKS = F // P
 SLOPE = 0.01
+ROOT_OF_ROWS = 64.0
 EPS = 1e-5
 
 PHASES = ((0, 1, 2), (3,))
@@ -56,7 +57,7 @@ def tile_attention_prop_pa_t_kernel(
         one = keep.tile([P, 1], F32)
         nc.vector.memset(one[:], 1.0)
         warm = keep.tile([P, 1], F32)
-        nc.scalar.activation(out=warm[:], in_=one[:], func=ACT.Sqrt)
+        nc.scalar.activation(out=warm[:], in_=one[:], func=ACT.Abs_reciprocal_sqrt)
 
         planes = keep.tile([P, PASSES1 + 1, F], U8, align_bytes=64)
         nc.vector.memset(planes[:].bitcast(I32), 0)
@@ -264,6 +265,7 @@ def tile_attention_prop_pa_t_kernel(
                 out=unread[:],
                 in_=h2t[:, fb, cols],
                 func=ACT.Square,
+                scale=ROOT_OF_ROWS,
                 accum_out=moments[:, 1, fb, group : group + 1],
             )
 
@@ -272,21 +274,26 @@ def tile_attention_prop_pa_t_kernel(
             nc.vector.tensor_reduce(
                 out=totals[:, :, s], in_=moments[:, :, s, :], axis=mybir.AxisListType.X, op=ALU.add
             )
-            nc.vector.tensor_mul(out=mean_sq[:, s], in0=totals[:, 0, s], in1=totals[:, 0, s])
-            nc.vector.scalar_tensor_tensor(
-                out=var[:, s], in0=totals[:, 1, s], scalar=float(ROWS), in1=mean_sq[:, s],
-                op0=ALU.mult, op1=ALU.subtract,
-            )
+            for fb in range(lo, hi):
+                c = slice(fb, fb + 1)
+                nc.vector.scalar_tensor_tensor(
+                    out=var[:, c], in0=totals[:, 0, c], scalar=totals[:, 0, c], in1=totals[:, 1, c],
+                    op0=ALU.mult, op1=ALU.subtract,
+                )
             nc.scalar.activation(
-                out=std[:, s], in_=var[:, s], func=ACT.Sqrt, scale=1.0 / (ROWS * ROWS), bias=eps_col[:]
+                out=std[:, s], in_=var[:, s], func=ACT.Abs_reciprocal_sqrt, scale=-1.0 / (ROWS * ROWS), bias=eps_col[:]
             )
-            nc.vector.reciprocal(out=gain[:, s], in_=std[:, s])
-            nc.vector.tensor_mul(out=gain[:, s], in0=gain[:, s], in1=vec_cols[:, F_BLOCKS + lo : F_BLOCKS + hi])
-            nc.vector.tensor_mul(out=shift[:, s], in0=totals[:, 0, s], in1=gain[:, s])
             nc.vector.scalar_tensor_tensor(
-                out=shift[:, s], in0=shift[:, s], scalar=-1.0 / ROWS,
-                in1=vec_cols[:, 2 * F_BLOCKS + lo : 2 * F_BLOCKS + hi], op0=ALU.mult, op1=ALU.add,
+                out=mean_sq[:, s], in0=totals[:, 0, s], scalar=-1.0 / ROWS,
+                in1=vec_cols[:, F_BLOCKS + lo : F_BLOCKS + hi], op0=ALU.mult, op1=ALU.mult,
             )
+            nc.vector.tensor_mul(out=gain[:, s], in0=std[:, s], in1=vec_cols[:, F_BLOCKS + lo : F_BLOCKS + hi])
+            for fb in range(lo, hi):
+                c = slice(fb, fb + 1)
+                nc.vector.scalar_tensor_tensor(
+                    out=shift[:, c], in0=mean_sq[:, c], scalar=std[:, c],
+                    in1=vec_cols[:, 2 * F_BLOCKS + fb : 2 * F_BLOCKS + fb + 1], op0=ALU.mult, op1=ALU.add,
+                )
 
         counts = {"bank": 0, "copy": 0, "norm": 0}
 

@@ -142,6 +142,7 @@ def tile_attention_prop_pa_t_kernel(
         h_scales = keep.tile([P, GROUPS, GROUP_ROWS], U8, align_bytes=64)
         h2t = keep.tile([P, F_BLOCKS, ROWS], F32)
         moments = keep.tile([P, 2, F_BLOCKS, GROUPS], F32)
+        nc.vector.memset(moments[:], 0.0)
         totals = keep.tile([P, 2, F_BLOCKS], F32)
         eps_col = keep.tile([P, 1], F32)
         nc.vector.tensor_scalar(out=eps_col[:], in0=one[:], scalar1=0.0, scalar2=EPS, op0=ALU.mult, op1=ALU.add)
@@ -260,10 +261,17 @@ def tile_attention_prop_pa_t_kernel(
                 op1=ALU.max,
                 accum_out=moments[:, 0, fb, group : group + 1],
             )
-            unread = work.tile([P, GROUP_ROWS], BF16, name="unread")
+            if group >= GROUPS - 2:
+                first = group
+            elif group % 2 == 1:
+                first = group - 1
+            else:
+                return
+            both = slice(first * GROUP_ROWS, (group + 1) * GROUP_ROWS)
+            unread = work.tile([P, 2 * GROUP_ROWS], BF16, name="unread")
             nc.scalar.activation(
-                out=unread[:],
-                in_=h2t[:, fb, cols],
+                out=unread[:, 0 : (group + 1 - first) * GROUP_ROWS],
+                in_=h2t[:, fb, both],
                 func=ACT.Square,
                 scale=ROOT_OF_ROWS,
                 accum_out=moments[:, 1, fb, group : group + 1],
@@ -305,7 +313,7 @@ def tile_attention_prop_pa_t_kernel(
                 "(p j) f -> p j f", j=4
             )
             for fb in blocks:
-                on_gpsimd = (not last) and counts["norm"] % NORM_GPSIMD_OF == 0
+                on_gpsimd = (not last) and counts["norm"] % 3 != 1
                 counts["norm"] += 1
                 engine = nc.gpsimd if on_gpsimd else nc.vector
                 engine.tensor_scalar(

@@ -313,12 +313,17 @@ def tile_attention_prop_pa_t_kernel(
                 "(p j) f -> p j f", j=4
             )
             for fb in blocks:
-                on_gpsimd = (not last) and counts["norm"] % 3 != 1
-                counts["norm"] += 1
-                engine = nc.gpsimd if on_gpsimd else nc.vector
+                if last:
+                    engine, span = nc.vector, cols
+                elif group < 2:
+                    engine, span = nc.vector, cols
+                elif group % 2 == 0:
+                    engine, span = nc.gpsimd, slice(group * GROUP_ROWS, (group + 2) * GROUP_ROWS)
+                else:
+                    continue
                 engine.tensor_scalar(
-                    out=h2t[:, fb, cols],
-                    in0=h2t[:, fb, cols],
+                    out=h2t[:, fb, span],
+                    in0=h2t[:, fb, span],
                     scalar1=gain[:, fb : fb + 1],
                     scalar2=shift[:, fb : fb + 1],
                     op0=ALU.mult,

from contextlib import ExitStack

import concourse.mybir as mybir
from concourse.masks import make_identity

F32 = mybir.dt.float32
BF16 = mybir.dt.bfloat16
I32 = mybir.dt.int32
U32 = mybir.dt.uint32
U8 = mybir.dt.uint8
FP8X4 = mybir.dt.float8_e4m3fn_x4
ALU = mybir.AluOpType
ACT = mybir.ActivationFunctionType

P = 128
ROWS = 4096
K1 = 1024
F = 512
K_PASS = 512
PASSES1 = K1 // K_PASS
PACK = 4
GROUP_ROWS = 4 * P
HALF_ROWS = 2 * P
GROUPS = ROWS // GROUP_ROWS
F_BLOCKS = F // P
SLOPE = 0.01
ROOT_OF_ROWS = 64.0
EPS = 1e-5

PHASES = ((0, 1, 2), (3,))
X_COPIES_ON_SCALAR = (3, 2)
LOADS = (0, "w1", 1, "w2", 2, 3, 4, 5, 6, 7)
PIECES = 1
LAG = 2
NORM_GPSIMD_OF = 2
COPY_SCALAR_OF = 2

FLOPS = 2 * ROWS * K1 * F + 2 * ROWS * F * F


def tile_attention_prop_pa_t_kernel(
    tc, x, w1_words, w1_scales, b1, w2_words, w2_scales, b2, gamma, beta, out
):
    nc = tc.nc
    with ExitStack() as stack:
        keep = stack.enter_context(tc.tile_pool(name="keep", bufs=1))
        x_pool = stack.enter_context(tc.tile_pool(name="x_pool", bufs=6))
        xg_pool = stack.enter_context(tc.tile_pool(name="xg_pool", bufs=4))
        xc_pool = stack.enter_context(tc.tile_pool(name="xc_pool", bufs=6))
        v_pool = stack.enter_context(tc.tile_pool(name="v_pool", bufs=3))
        hg_pool = stack.enter_context(tc.tile_pool(name="hg_pool", bufs=2))
        work = stack.enter_context(tc.tile_pool(name="work", bufs=4))
        ps_xt = stack.enter_context(tc.psum_pool(name="ps_xt", bufs=2))
        ps_acc1 = stack.enter_context(tc.psum_pool(name="ps_acc1", bufs=3))
        ps_acc2 = stack.enter_context(tc.psum_pool(name="ps_acc2", bufs=3))

        one = keep.tile([P, 1], F32)
        nc.vector.memset(one[:], 1.0)
        warm = keep.tile([P, 1], F32)
        nc.scalar.activation(out=warm[:], in_=one[:], func=ACT.Abs_reciprocal_sqrt)

        planes = keep.tile([P, PASSES1 + 1, F], U8, align_bytes=64)
        nc.vector.memset(planes[:].bitcast(I32), 0)
        ident_f32 = keep.tile([P, P], F32)
        make_identity(nc, ident_f32[:])

        for q in range(4):
            nc.sync.dma_start(
                out=planes[32 * q : 32 * q + 4, 0:PASSES1, :].bitcast(I32),
                in_=w1_scales[:, 4 * q : 4 * q + 4, :].rearrange("g r n -> r g n").bitcast(I32),
            )

        x_tiles = []

        def load_x(group, in_pieces):
            x_sb = x_pool.tile([P, 4, K1], BF16, name="x_sb")
            rows = x[group * GROUP_ROWS : (group + 1) * GROUP_ROWS, :].rearrange("(p j) k -> p j k", j=4)
            if in_pieces:
                for g in range(PASSES1):
                    ks = slice(g * K_PASS, (g + 1) * K_PASS)
                    for half in range(2):
                        js = slice(2 * half, 2 * half + 2)
                        nc.sync.dma_start(out=x_sb[:, js, ks], in_=rows[:, js, ks])
            else:
                nc.sync.dma_start(out=x_sb[:], in_=rows)
            x_tiles.append(x_sb)

        w1_raw = keep.tile([P, PASSES1, F], U32)
        w2_sb = keep.tile([P, F], U32, align_bytes=64)

        def load_w1():
            nc.sync.dma_start(
                out=w1_raw[:].bitcast(I32),
                in_=w1_words.rearrange("g p n t -> p g (n t)").bitcast(I32),
            )

        def load_w2():
            for q in range(4):
                nc.sync.dma_start(
                    out=planes[32 * q : 32 * q + 4, PASSES1, :].bitcast(I32),
                    in_=w2_scales[0, 4 * q : 4 * q + 4, :].bitcast(I32),
                )
            nc.sync.dma_start(
                out=w2_sb[:].bitcast(I32),
                in_=w2_words[0].rearrange("p n t -> p (n t)").bitcast(I32),
            )

        for what in LOADS:
            if what == "w1":
                load_w1()
            elif what == "w2":
                load_w2()
            else:
                load_x(what, what < PIECES)

        b1_bf = keep.tile([P, PACK], BF16)
        nc.gpsimd.dma_start(out=b1_bf[:], in_=b1.rearrange("(p t) -> p t", t=PACK))
        vec_rows = keep.tile([P, P], BF16)
        nc.vector.memset(vec_rows[:], 0.0)
        for i, vec in enumerate((b2, gamma, beta)):
            nc.gpsimd.dma_start(
                out=vec_rows[F_BLOCKS * i : F_BLOCKS * (i + 1), :],
                in_=vec.rearrange("(f c) -> f c", c=P),
            )
        ident_bf16 = keep.tile([P, P], BF16)
        make_identity(nc, ident_bf16[:])

        planes1 = keep.tile([P, PASSES1, F], U8, align_bytes=64)
        nc.vector.tensor_copy(
            out=planes1[:].rearrange("p g (t m) -> p g m t", t=PACK),
            in_=planes[:, 0:PASSES1, :].rearrange("p g (m t) -> p g m t", t=PACK),
        )
        w1_sb = keep.tile([P, PASSES1, F], U32, align_bytes=64)
        nc.vector.tensor_copy(
            out=w1_sb[:].bitcast(I32).rearrange("p g (t m) -> p g t m", t=PACK),
            in_=w1_raw[:].bitcast(I32).rearrange("p g (m t) -> p g t m", t=PACK),
        )
        b1_cols = keep.tile([P, PACK], F32)
        nc.vector.tensor_copy(out=b1_cols[:], in_=b1_bf[:])

        h_codes = keep.tile([P, GROUPS, GROUP_ROWS], U32, align_bytes=64)
        h_scales = keep.tile([P, GROUPS, GROUP_ROWS], U8, align_bytes=64)
        h2t = keep.tile([P, F_BLOCKS, ROWS], F32)
        moments = keep.tile([P, 2, F_BLOCKS, GROUPS], F32)
        nc.vector.memset(moments[:], 0.0)
        totals = keep.tile([P, 2, F_BLOCKS], F32)
        eps_col = keep.tile([P, 1], F32)
        nc.vector.tensor_scalar(out=eps_col[:], in0=one[:], scalar1=0.0, scalar2=EPS, op0=ALU.mult, op1=ALU.add)
        vec_cols = keep.tile([P, 3 * F_BLOCKS], F32)
        b2_slope = keep.tile([P, F_BLOCKS], F32)
        var = keep.tile([P, F_BLOCKS], F32)
        mean_sq = keep.tile([P, F_BLOCKS], F32)
        std = keep.tile([P, F_BLOCKS], F32)
        gain = keep.tile([P, F_BLOCKS], F32)
        shift = keep.tile([P, F_BLOCKS], F32)

        x_grouped = {}
        x_codes = {}
        v_tiles = {}
        h_grouped = {}

        def vectors_to_columns():
            vec_ps = ps_acc2.tile([P, P], BF16, name="acc2")
            nc.tensor.transpose(vec_ps[:], vec_rows[:], ident_bf16[:])
            nc.vector.tensor_copy(out=vec_cols[:], in_=vec_ps[:, 0 : 3 * F_BLOCKS])
            nc.vector.tensor_scalar_mul(out=b2_slope[:], in0=vec_cols[:, 0:F_BLOCKS], scalar1=SLOPE)

        def transpose_x(group):
            x_words = x_tiles[group][:].bitcast(F32)
            for g in range(PASSES1):
                grouped = xg_pool.tile([P, GROUP_ROWS, PACK], BF16, name="x_grouped", align_bytes=64)
                for half in range(2):
                    xt = ps_xt.tile([P, 2, HALF_ROWS], F32, name="xt")
                    for jj in range(2):
                        j = 2 * half + jj
                        for u in range(2):
                            nc.tensor.transpose(
                                xt[:, u, jj * P : (jj + 1) * P],
                                x_words[:, j, 256 * g + u : 256 * (g + 1) : 2],
                                ident_f32[:],
                            )
                    dst = grouped[:, half * HALF_ROWS : (half + 1) * HALF_ROWS, :].bitcast(F32)
                    src = xt[:].rearrange("p u r -> p r u")
                    if 2 * g + half < X_COPIES_ON_SCALAR[group % 2]:
                        nc.scalar.copy(out=dst, in_=src)
                    else:
                        nc.vector.tensor_copy(out=dst, in_=src)
                x_grouped[(group, g)] = grouped

        def quantise_x(group):
            for g in range(PASSES1):
                grouped = x_grouped.pop((group, g))
                codes = xc_pool.tile([P, GROUP_ROWS], U32, name="x_code", align_bytes=64)
                scales = xc_pool.tile([P, GROUP_ROWS], U8, name="x_scale", align_bytes=64)
                nc.vector.quantize_mx(
                    out=codes[:].bitcast(FP8X4),
                    scales=scales[:],
                    in_=grouped[:].rearrange("p r t -> p (r t)"),
                )
                x_codes[(group, g)] = (codes, scales)

        def layer1(group):
            v = v_pool.tile([P, PACK, GROUP_ROWS], F32, name="v")
            for t in range(PACK):
                feats = slice(t * P, (t + 1) * P)
                acc1 = ps_acc1.tile([P, GROUP_ROWS], F32, name="acc1")
                for g in range(PASSES1):
                    codes, scales = x_codes[(group, g)]
                    nc.tensor.matmul_mx(
                        out=acc1[:],
                        lhsT=w1_sb[:, g, feats].bitcast(FP8X4),
                        lhsT_scale=planes1[:, g, feats],
                        rhs=codes[:].bitcast(FP8X4),
                        rhs_scale=scales[:],
                        start=(g == 0),
                        stop=(g == PASSES1 - 1),
                    )
                nc.scalar.activation(
                    out=v[:, t, :], in_=acc1[:], func=ACT.Identity, bias=b1_cols[:, t : t + 1]
                )
            v_tiles[group] = v

        def leaky1(group):
            v_rt = v_tiles.pop(group)[:].rearrange("p t r -> p r t")
            grouped = hg_pool.tile([P, GROUP_ROWS, PACK], BF16, name="h_grouped", align_bytes=64)
            nc.vector.scalar_tensor_tensor(
                out=grouped[:], in0=v_rt, scalar=SLOPE, in1=v_rt, op0=ALU.mult, op1=ALU.max
            )
            h_grouped[group] = grouped

        def quantise_h(group):
            nc.vector.quantize_mx(
                out=h_codes[:, group, :].bitcast(FP8X4),
                scales=h_scales[:, group, :],
                in_=h_grouped.pop(group)[:].rearrange("p r t -> p (r t)"),
            )

        def layer2(fb, group):
            cols = slice(group * GROUP_ROWS, (group + 1) * GROUP_ROWS)
            feats = slice(fb * P, (fb + 1) * P)
            acc2 = ps_acc2.tile([P, GROUP_ROWS], F32, name="acc2")
            nc.tensor.matmul_mx(
                out=acc2[:],
                lhsT=w2_sb[:, feats].bitcast(FP8X4),
                lhsT_scale=planes[:, PASSES1, feats],
                rhs=h_codes[:, group, :].bitcast(FP8X4),
                rhs_scale=h_scales[:, group, :],
                start=True,
                stop=True,
            )
            low = work.tile([P, GROUP_ROWS], F32, name="low")
            nc.scalar.activation(
                out=low[:], in_=acc2[:], func=ACT.Identity, scale=SLOPE, bias=b2_slope[:, fb : fb + 1]
            )
            nc.vector.scalar_tensor_tensor(
                out=h2t[:, fb, cols],
                in0=acc2[:],
                scalar=vec_cols[:, fb : fb + 1],
                in1=low[:],
                op0=ALU.add,
                op1=ALU.max,
                accum_out=moments[:, 0, fb, group : group + 1],
            )
            if group >= GROUPS - 2:
                first = group
            elif group % 2 == 1:
                first = group - 1
            else:
                return
            both = slice(first * GROUP_ROWS, (group + 1) * GROUP_ROWS)
            unread = work.tile([P, 2 * GROUP_ROWS], BF16, name="unread")
            nc.scalar.activation(
                out=unread[:, 0 : (group + 1 - first) * GROUP_ROWS],
                in_=h2t[:, fb, both],
                func=ACT.Square,
                scale=ROOT_OF_ROWS,
                accum_out=moments[:, 1, fb, group : group + 1],
            )

        def statistics(lo, hi):
            s = slice(lo, hi)
            nc.vector.tensor_reduce(
                out=totals[:, :, s], in_=moments[:, :, s, :], axis=mybir.AxisListType.X, op=ALU.add
            )
            for fb in range(lo, hi):
                c = slice(fb, fb + 1)
                nc.vector.scalar_tensor_tensor(
                    out=var[:, c], in0=totals[:, 0, c], scalar=totals[:, 0, c], in1=totals[:, 1, c],
                    op0=ALU.mult, op1=ALU.subtract,
                )
            nc.scalar.activation(
                out=std[:, s], in_=var[:, s], func=ACT.Abs_reciprocal_sqrt, scale=-1.0 / (ROWS * ROWS), bias=eps_col[:]
            )
            nc.vector.scalar_tensor_tensor(
                out=mean_sq[:, s], in0=totals[:, 0, s], scalar=-1.0 / ROWS,
                in1=vec_cols[:, F_BLOCKS + lo : F_BLOCKS + hi], op0=ALU.mult, op1=ALU.mult,
            )
            nc.vector.tensor_mul(out=gain[:, s], in0=std[:, s], in1=vec_cols[:, F_BLOCKS + lo : F_BLOCKS + hi])
            for fb in range(lo, hi):
                c = slice(fb, fb + 1)
                nc.vector.scalar_tensor_tensor(
                    out=shift[:, c], in0=mean_sq[:, c], scalar=std[:, c],
                    in1=vec_cols[:, 2 * F_BLOCKS + fb : 2 * F_BLOCKS + fb + 1], op0=ALU.mult, op1=ALU.add,
                )

        counts = {"bank": 0, "copy": 0, "norm": 0}

        def output(blocks, group, last):
            cols = slice(group * GROUP_ROWS, (group + 1) * GROUP_ROWS)
            lo = blocks[0]
            stage = x_pool.tile([P, 4, len(blocks) * P], F32, name="x_sb")
            rows = out[group * GROUP_ROWS : (group + 1) * GROUP_ROWS, lo * P : (lo + len(blocks)) * P].rearrange(
                "(p j) f -> p j f", j=4
            )
            for fb in blocks:
                if last:
                    engine, span = nc.vector, cols
                elif group < 2:
                    engine, span = nc.vector, cols
                elif group % 2 == 0:
                    engine, span = nc.gpsimd, slice(group * GROUP_ROWS, (group + 2) * GROUP_ROWS)
                else:
                    continue
                engine.tensor_scalar(
                    out=h2t[:, fb, span],
                    in0=h2t[:, fb, span],
                    scalar1=gain[:, fb : fb + 1],
                    scalar2=shift[:, fb : fb + 1],
                    op0=ALU.mult,
                    op1=ALU.add,
                )
            for fb in blocks:
                if counts["bank"] % 5 < 2:
                    ot = ps_xt.tile([P, 4, P], F32, name="xt")
                else:
                    ot = ps_acc1.tile([P, 4, P], F32, name="acc1")
                counts["bank"] += 1
                for j in range(4):
                    first = group * GROUP_ROWS + j * P
                    nc.tensor.transpose(ot[:, j, :], h2t[:, fb, first : first + P], ident_f32[:])
                dst = stage[:, :, (fb - lo) * P : (fb - lo + 1) * P]
                if counts["copy"] % COPY_SCALAR_OF == 0:
                    nc.scalar.copy(out=dst, in_=ot[:])
                else:
                    nc.vector.tensor_copy(out=dst, in_=ot[:])
                counts["copy"] += 1
            nc.sync.dma_start(out=rows, in_=stage[:])

        for step in range(GROUPS + 3):
            if step < GROUPS:
                transpose_x(step)
            if 0 <= step - 1 < GROUPS:
                quantise_x(step - 1)
                layer1(step - 1)
            if 0 <= step - 2 < GROUPS:
                leaky1(step - 2)
            if step == 3:
                vectors_to_columns()
            if 0 <= step - 3 < GROUPS:
                quantise_h(step - 3)
                for fb in PHASES[0]:
                    layer2(fb, step - 3)

        statistics(PHASES[0][0], PHASES[0][-1] + 1)
        for i in range(1, len(PHASES)):
            for group in range(GROUPS):
                for fb in PHASES[i]:
                    layer2(fb, group)
                if group >= LAG:
                    output(PHASES[i - 1], group - LAG, False)
            statistics(PHASES[i][0], PHASES[i][-1] + 1)
            for group in range(GROUPS - LAG, GROUPS):
                output(PHASES[i - 1], group, False)
        for group in range(GROUPS):
            output(PHASES[-1], group, True)
